import numpy as np
import ml_dtypes


def mxq(x, axis, fmt="e4m3"):
    dtype, down = {"e4m3": (ml_dtypes.float8_e4m3fn, 7), "e5m2": (ml_dtypes.float8_e5m2, 14)}[fmt]
    v = np.moveaxis(np.asarray(x, np.float32).astype(ml_dtypes.bfloat16).astype(np.float64), axis, -1)
    blocks = v.reshape(v.shape[:-1] + (-1, 32))
    amax = np.abs(blocks).max(-1, keepdims=True)
    byte = np.maximum(np.where(amax > 0, np.frexp(amax)[1] - 1 + 127, 0) - down, 1)
    scale = np.exp2(byte - 127.0)
    codes = (blocks / scale).astype(np.float32).astype(dtype).astype(np.float64)
    return np.moveaxis((codes * scale).reshape(v.shape), -1, axis)


WIDE = False


def mx_kscale(k):
    if not WIDE:
        return np.ones(k)
    levels = np.array([10, -10, 5, -5, 0])
    a = np.random.permutation(np.resize(levels, k // 512 * 4)).reshape(k // 512, 4)
    idx = np.arange(k)
    return np.exp2(a[idx // 512, idx % 128 // 32])


BF16 = ml_dtypes.bfloat16


def bf(x):
    return np.asarray(x, np.float32).astype(BF16)


def f64(x):
    return np.asarray(x).astype(np.float64)


E2M1 = np.array([0.0, 0.5, 1.0, 1.5, 2.0, 3.0, 4.0, 6.0, -0.0, -0.5, -1.0, -1.5, -2.0, -3.0, -4.0, -6.0])


def pack_weight(w, fmt):
    k, n = w.shape
    w = f64(bf(w)).reshape(k // 32, 32, n)
    amax = np.abs(w).max(1)
    if fmt == "e4m3":
        byte = np.frexp(amax)[1] - 1 + 127 - 7
    else:
        mant, ex = np.frexp(amax / 6.0)
        byte = np.where(mant > 0.5, ex, ex - 1) + 127
    byte = np.clip(np.where(amax > 0, byte, 1), 1, 254)
    scaled = (w * np.exp2(127.0 - byte)[:, None, :]).reshape(k, n).astype(np.float32)
    by_word = np.ascontiguousarray(scaled.reshape(k // 512, 128, 4, n).transpose(0, 1, 3, 2))
    if fmt == "e4m3":
        words = by_word.astype(ml_dtypes.float8_e4m3fn).view(np.uint8)
    else:
        c = by_word.astype(ml_dtypes.float4_e2m1fn).view(np.uint8) & 0xF
        words = c[..., 0::2] | (c[..., 1::2] << 4)
    return np.ascontiguousarray(words), np.ascontiguousarray(byte.astype(np.uint8).reshape(k // 512, 16, n))


def unpack_weight(words, scales, fmt):
    g, p, n, _ = words.shape
    if fmt == "e4m3":
        vals = np.ascontiguousarray(words).view(ml_dtypes.float8_e4m3fn).astype(np.float64)
    else:
        nib = np.empty((g, p, n, 4), np.uint8)
        nib[..., 0::2] = words & 0xF
        nib[..., 1::2] = words >> 4
        vals = E2M1[nib]
    vals = vals * np.repeat(np.exp2(scales.astype(np.float64) - 127.0), 8, axis=1)[..., None]
    return vals.transpose(0, 1, 3, 2).reshape(g * 512, n)


B, IN, OUT = 256, 4096, 4096
EPS = 1e-5


def setup_inputs():
    s = mx_kscale(IN)
    x = bf(np.random.standard_normal((B, IN)) * s)
    weight = np.random.standard_normal((OUT, IN)) / np.sqrt(IN) / s[None, :]
    weight_words, weight_scales = pack_weight(np.ascontiguousarray(weight.T), "e4m3")
    return {"x": x,
            "weight_words": weight_words,
            "weight_scales": weight_scales,
            "bias": bf(np.random.standard_normal(OUT) * 0.1),
            "bn_weight": bf(1.0 + 0.1 * np.random.standard_normal(OUT)),
            "bn_bias": bf(np.random.standard_normal(OUT) * 0.1),
            "bn_mean": bf(np.random.standard_normal(OUT) * 0.1),
            "bn_var": bf(np.random.uniform(0.5, 1.5, OUT)),
            "gn_weight": bf(1.0 + 0.25 * np.sqrt(OUT) * np.random.standard_normal(OUT)),
            "gn_bias": bf(0.15 + 0.1 * np.random.standard_normal(OUT))}


def reference(x, weight_words, weight_scales, bias, bn_weight, bn_bias, bn_mean, bn_var, gn_weight, gn_bias):
    y = (mxq(f64(x), 1, "e4m3") @ unpack_weight(weight_words, weight_scales, "e4m3")) + f64(bias)
    y = (y - f64(bn_mean)) / np.sqrt(f64(bn_var) + EPS) * f64(bn_weight) + f64(bn_bias)
    y = y * 0.5 * (1.0 + np.tanh(0.797885 * y + 0.035677 * y * y * y))
    mean = np.mean(y, axis=1, keepdims=True)
    var = np.mean(y * y, axis=1, keepdims=True) - mean * mean
    gn = (y - mean) / np.sqrt(var + EPS) * f64(gn_weight) + f64(gn_bias)
    out = np.maximum(np.mean(gn, axis=1, keepdims=True), 0.0)
    return out

@@ -1,0 +1,306 @@
+from contextlib import ExitStack
+
+import concourse.mybir as mybir
+from concourse.masks import make_identity
+
+F32 = mybir.dt.float32
+BF16 = mybir.dt.bfloat16
+U8 = mybir.dt.uint8
+U32 = mybir.dt.uint32
+I32 = mybir.dt.int32
+FP8X4 = mybir.dt.float8_e4m3fn_x4
+ACT = mybir.ActivationFunctionType
+ALU = mybir.AluOpType
+AX = mybir.AxisListType
+
+P = 128
+ROWS = 256
+K = 4096
+N = 4096
+PASSES = K // 512
+EPS = 1e-5
+C1 = 0.797885
+C2 = 0.035677
+KAPPA = C1 / C2
+K1 = 1.0 / (2 * N)
+K2 = 1.0 / (4 * N)
+FLOPS = 2 * ROWS * K * N
+
+CHUNKS = [(4, 2)] * 7 + [(2, 4), (1, 4), (1, 4)]
+NC = len(CHUNKS)
+PINNED = True
+LEAD = 4
+
+
+def tile_modelnew_w_kernel(
+    tc, x, weight_words, weight_scales, bias, bn_weight, bn_bias, bn_mean, bn_var, gn_weight, gn_bias, out
+):
+    nc = tc.nc
+    assert sum(ch[0] for ch in CHUNKS) * P == N
+    starts = [sum(ch[0] for ch in CHUNKS[:c]) for c in range(NC)]
+    with ExitStack() as ctx:
+        if PINNED:
+            ctx.enter_context(tc.manual_schedule())
+        keep = ctx.enter_context(tc.tile_pool(name="keep", bufs=1))
+        work = ctx.enter_context(tc.tile_pool(name="work", bufs=3))
+        psum = ctx.enter_context(tc.psum_pool(name="psum", bufs=8))
+
+        planes = keep.tile([P, 2, N], U8, align_bytes=64, name="planes")
+        nc.vector.memset(planes[:].rearrange("p s n -> p (s n)").bitcast(I32), 0)
+        gwrow = keep.tile([P, N], BF16, name="gwrow")
+        nc.vector.memset(gwrow[:].bitcast(I32), 0)
+        vecs = keep.tile([P, 2, P], BF16, name="vecs")
+        nc.vector.memset(vecs[96:128, 1, :], 0.0)
+        one = keep.tile([P, 1], F32, name="one")
+        nc.vector.memset(one[:], 1.0)
+        stv = keep.tile([P, 3, 2, NC], F32, name="stv")
+        nc.vector.memset(stv[:], 0.0)
+
+        ident = keep.tile([P, P], F32, name="ident")
+        make_identity(nc, ident[:])
+
+        xv = x.rearrange("(m p) k -> p m k", p=P)
+        xs = []
+        for q in range(4):
+            xq = keep.tile([P, 2, 1024], BF16, name="x%d" % q)
+            nc.sync.dma_start(out=xq[:], in_=xv[:, :, 1024 * q : 1024 * (q + 1)])
+            xs.append(xq)
+        for i, v in enumerate([bias, bn_weight, bn_bias, bn_mean, bn_var, gn_weight, gn_bias]):
+            r0 = 32 * (i % 4)
+            queue = nc.scalar if i < 4 else nc.gpsimd
+            queue.dma_start(out=vecs[r0 : r0 + 32, i // 4, :], in_=v.rearrange("(j p) -> j p", p=P))
+            if i == 4:
+                nc.gpsimd.dma_start(out=gwrow[0:1, :], in_=gn_weight.rearrange("(o n) -> o n", o=1))
+        ones_bf = keep.tile([P, P], BF16, name="ones_bf")
+        nc.gpsimd.memset(ones_bf[:], K1)
+        ones_n = keep.tile([P, P], F32, name="ones_n")
+        nc.gpsimd.memset(ones_n[:], 1.0 / N)
+        res = keep.tile([P, P], F32, name="res")
+        nc.gpsimd.memset(res[:], 0.0)
+        for s in range(2):
+            for quad in range(4):
+                nc.sync.dma_start(
+                    out=planes[32 * quad : 32 * quad + 16, s, :].bitcast(I32),
+                    in_=weight_scales[4 * s : 4 * s + 4, 4 * quad : 4 * quad + 4, :].bitcast(I32),
+                )
+        wv = weight_words.rearrange("g p n t -> p g (n t)")
+        wtiles = []
+        for c, (tiles, gd) in enumerate(CHUNKS):
+            cols = tiles * P
+            n0 = starts[c] * P
+            pieces = []
+            for d in range(PASSES // gd):
+                wt = keep.tile([P, gd, cols], U32, align_bytes=64, name="w%d_%d" % (c, d))
+                nc.sync.dma_start(
+                    out=wt[:].bitcast(I32),
+                    in_=wv[:, d * gd : (d + 1) * gd, 4 * n0 : 4 * (n0 + cols)].bitcast(I32),
+                )
+                pieces.append(wt)
+            wtiles.append(pieces)
+
+        junk0 = keep.tile([P, 1], F32, name="junk0")
+        nc.scalar.activation(out=junk0[:], in_=one[:], func=ACT.Sqrt)
+
+        xc = keep.tile([P, PASSES, ROWS], U32, align_bytes=64, name="xc")
+        xsc = keep.tile([P, PASSES, ROWS], U8, align_bytes=64, name="xsc")
+        for g in range(PASSES):
+            xt = psum.tile([P, 2, ROWS], F32, tag="bank", name="xt%d" % g)
+            for m in range(2):
+                words = xs[g // 2][:, m, :].bitcast(F32)
+                base = 256 * (g % 2)
+                for u in range(2):
+                    nc.tensor.transpose(xt[:, u, m * P : (m + 1) * P], words[:, base + u : base + 256 : 2], ident[:])
+            grp = work.tile([P, 4 * ROWS], BF16, align_bytes=64, tag="grp", name="grp%d" % g)
+            nc.scalar.copy(
+                out=grp[:].bitcast(F32).rearrange("p (r u) -> p r u", u=2),
+                in_=xt[:].rearrange("p u r -> p r u"),
+            )
+            nc.vector.quantize_mx(out=xc[:, g, :].bitcast(FP8X4), scales=xsc[:, g, :], in_=grp[:])
+
+        vecf = keep.tile([P, 2, P], F32, name="vecf")
+        nc.vector.tensor_copy(out=vecf[:], in_=vecs[:])
+        vps = psum.tile([P, 2, P], F32, tag="bank", name="vps")
+        for h in range(2):
+            nc.tensor.transpose(vps[:, h, :], vecf[:, h, :], ident[:])
+        vt = keep.tile([P, 2 * P], F32, name="vt")
+        nc.vector.tensor_copy(out=vt[:], in_=vps[:].rearrange("p h j -> p (h j)"))
+        v_bias, v_bnw, v_bnb, v_bnm = vt[:, 0:32], vt[:, 32:64], vt[:, 64:96], vt[:, 96:128]
+        v_var = vt[:, 128:160]
+        ve = keep.tile([P, 32], F32, name="ve")
+        nc.vector.tensor_scalar_add(out=ve[:], in0=v_var, scalar1=EPS)
+        sd = keep.tile([P, 32], F32, name="sd")
+        nc.scalar.activation(out=sd[:], in_=ve[:], func=ACT.Sqrt)
+        junk1 = keep.tile([P, 1], F32, name="junk1")
+        nc.scalar.activation(out=junk1[:], in_=sd[:, 0:1], func=ACT.Tanh)
+        rs = keep.tile([P, 32], F32, name="rs")
+        nc.vector.reciprocal(out=rs[:], in_=sd[:])
+        ga = keep.tile([P, 32], F32, name="ga")
+        nc.vector.tensor_tensor(out=ga[:], in0=v_bnw, in1=rs[:], op=ALU.mult)
+        gd0 = keep.tile([P, 32], F32, name="gd0")
+        nc.vector.tensor_tensor(out=gd0[:], in0=v_bias, in1=v_bnm, op=ALU.subtract)
+        gd1 = keep.tile([P, 32], F32, name="gd1")
+        nc.vector.tensor_tensor(out=gd1[:], in0=gd0[:], in1=ga[:], op=ALU.mult)
+        gb = keep.tile([P, 32], F32, name="gb")
+        nc.vector.tensor_tensor(out=gb[:], in0=gd1[:], in1=v_bnb, op=ALU.add)
+        gsum = keep.tile([P, 2], F32, name="gsum")
+        nc.vector.tensor_reduce(
+            out=gsum[:], in_=vt[:, 160:224].rearrange("p (v j) -> p v j", v=2), axis=AX.X, op=ALU.add
+        )
+
+        gwbc = keep.tile([P, N], BF16, name="gwbc")
+        for h in range(4):
+            gps = psum.tile([P, 1024], BF16, tag="bank", name="gps%d" % h)
+            for i in range(2):
+                lo = (2 * h + i) * 512
+                nc.tensor.matmul(
+                    out=gps[:, i * 512 : (i + 1) * 512], lhsT=ones_bf[:], rhs=gwrow[:, lo : lo + 512], start=True, stop=True
+                )
+            nc.scalar.copy(out=gwbc[:, h * 1024 : (h + 1) * 1024], in_=gps[:])
+        cps = psum.tile([P, 2], F32, tag="bank", name="cps")
+        nc.tensor.matmul(out=cps[:], lhsT=ones_n[:], rhs=gsum[:], start=True, stop=True)
+        cst = keep.tile([P, 2], F32, name="cst")
+        nc.vector.tensor_scalar(out=cst[:, 0:1], in0=cps[:, 0:1], scalar1=-K1, scalar2=None, op0=ALU.mult)
+        nc.vector.tensor_copy(out=cst[:, 1:2], in_=cps[:, 1:2])
+
+        st2 = keep.tile([P, 2, NC - 1], F32, name="st2")
+        junk_s = keep.tile([P, 512], F32, name="junk_s")
+        junk_v = keep.tile([P, 512], F32, name="junk_v")
+        mx = {}
+        zs = {}
+        zts = {}
+        es = {}
+
+        def pass_order(c):
+            tiles = CHUNKS[c][0]
+            early = [(g, t) for g in range(PASSES - 2) for t in range(tiles)]
+            late = [(g, t) for t in range(tiles) for g in (PASSES - 2, PASSES - 1)]
+            return early + late
+
+        def passes(c, todo):
+            tiles, gd = CHUNKS[c]
+            if c not in mx:
+                banks = []
+                for t in range(tiles):
+                    bank = psum.tile([P, ROWS], F32, tag="bank", name="mx%d_%d" % (c, t))
+                    banks.append(bank)
+                mx[c] = banks
+            for g, t in todo:
+                wt = wtiles[c][g // gd]
+                s, kk = divmod(g, 4)
+                n0 = (starts[c] + t) * P
+                nc.tensor.matmul_mx(
+                    out=mx[c][t][:],
+                    lhsT=wt[:, g % gd, t * P : (t + 1) * P].bitcast(FP8X4),
+                    lhsT_scale=planes[4 * kk : P, s, n0 : n0 + P],
+                    rhs=xc[:, g, :].bitcast(FP8X4),
+                    rhs_scale=xsc[:, g, :],
+                    start=(g == 0),
+                    stop=(g == PASSES - 1),
+                )
+
+        def evac(c):
+            tiles = CHUNKS[c][0]
+            zl = []
+            for t in range(tiles):
+                j = starts[c] + t
+                z = work.tile([P, ROWS], F32, tag="z", bufs=8, name="z%d" % j)
+                if t % 2 == 0:
+                    nc.scalar.activation(
+                        out=z[:], in_=mx[c][t][:], func=ACT.Identity, bias=gb[:, j : j + 1], scale=ga[:, j : j + 1]
+                    )
+                else:
+                    nc.vector.tensor_scalar(
+                        out=z[:], in0=mx[c][t][:], scalar1=ga[:, j : j + 1], scalar2=gb[:, j : j + 1],
+                        op0=ALU.mult, op1=ALU.add,
+                    )
+                zl.append(z)
+            zs[c] = zl
+
+        def transposes(c):
+            tiles = CHUNKS[c][0]
+            zl = []
+            for m in range(2):
+                zt = psum.tile([P, 512], F32, tag="bank", name="zt%d_%d" % (c, m))
+                for t in range(tiles):
+                    nc.tensor.transpose(zt[:, t * P : (t + 1) * P], zs[c][t][:, m * P : (m + 1) * P], ident[:])
+                zl.append(zt)
+            zts[c] = zl
+
+        def mainops(c):
+            w = CHUNKS[c][0] * P
+            el = []
+            for m in range(2):
+                e = work.tile([P, 512], F32, tag="e", bufs=6, name="e%d_%d" % (c, m))
+                nc.scalar.activation(out=e[:, :w], in_=zts[c][m][:, :w], func=ACT.Square)
+                el.append(e)
+            es[c] = el
+            for m in range(2):
+                nc.vector.scalar_tensor_tensor(
+                    out=el[m][:, :w], in0=el[m][:, :w], scalar=KAPPA, in1=zts[c][m][:, :w], op0=ALU.add, op1=ALU.mult
+                )
+            for m in range(2):
+                nc.scalar.activation(out=el[m][:, :w], in_=el[m][:, :w], func=ACT.Tanh, scale=C2)
+            for m in range(2):
+                nc.vector.scalar_tensor_tensor(
+                    out=el[m][:, :w], in0=el[m][:, :w], scalar=1.0, in1=zts[c][m][:, :w], op0=ALU.add, op1=ALU.mult,
+                    accum_out=stv[:, 0, m, c : c + 1],
+                )
+
+        def tailops(c):
+            w = CHUNKS[c][0] * P
+            n0 = starts[c] * P
+            for m in range(2):
+                e = es[c][m]
+                if c < NC - 1:
+                    nc.scalar.activation(out=junk_s[:, :w], in_=e[:, :w], func=ACT.Square, accum_out=st2[:, m, c : c + 1])
+                else:
+                    nc.vector.scalar_tensor_tensor(
+                        out=junk_v[:, :w], in0=e[:, :w], scalar=1.0, in1=e[:, :w], op0=ALU.mult, op1=ALU.mult,
+                        accum_out=stv[:, 2, m, c : c + 1],
+                    )
+                nc.vector.scalar_tensor_tensor(
+                    out=junk_v[:, :w], in0=e[:, :w], scalar=1.0, in1=gwbc[:, n0 : n0 + w], op0=ALU.mult, op1=ALU.mult,
+                    accum_out=stv[:, 1, m, c : c + 1],
+                )
+
+        passes(0, pass_order(0))
+        for c in range(NC):
+            evac(c)
+            if c + 1 < NC:
+                passes(c + 1, pass_order(c + 1)[:LEAD])
+            transposes(c)
+            if c >= 1:
+                tailops(c - 1)
+            mainops(c)
+            if c + 1 < NC:
+                passes(c + 1, pass_order(c + 1)[LEAD:])
+        junk2 = keep.tile([P, 1], F32, name="junk2")
+        nc.scalar.activation(out=junk2[:], in_=one[:], func=ACT.Sqrt)
+        nc.vector.tensor_reduce(out=stv[:, 2, :, 0], in_=st2[:], axis=AX.X, op=ALU.add)
+        tailops(NC - 1)
+
+        r = keep.tile([P, 6], F32, name="r")
+        nc.vector.tensor_reduce(out=r[:], in_=stv[:].rearrange("p w m c -> p (w m) c"), axis=AX.X, op=ALU.add)
+        s1, s3, s2 = r[:, 0:2], r[:, 2:4], r[:, 4:6]
+        t2 = keep.tile([P, 2], F32, name="t2")
+        nc.vector.tensor_scalar(out=t2[:], in0=s2, scalar1=K2, scalar2=EPS, op0=ALU.mult, op1=ALU.add)
+        msq = keep.tile([P, 2], F32, name="msq")
+        nc.vector.scalar_tensor_tensor(out=msq[:], in0=s1, scalar=K1 * K1, in1=s1, op0=ALU.mult, op1=ALU.mult)
+        var = keep.tile([P, 2], F32, name="var")
+        nc.vector.tensor_tensor(out=var[:], in0=t2[:], in1=msq[:], op=ALU.subtract)
+        sd2 = keep.tile([P, 2], F32, name="sd2")
+        nc.scalar.activation(out=sd2[:], in_=var[:], func=ACT.Sqrt)
+        num = keep.tile([P, 2], F32, name="num")
+        nc.vector.scalar_tensor_tensor(out=num[:], in0=s1, scalar=cst[:, 0:1], in1=s3, op0=ALU.mult, op1=ALU.add)
+        rstd = keep.tile([P, 2], F32, name="rstd")
+        nc.vector.reciprocal(out=rstd[:], in_=sd2[:])
+        prod = keep.tile([P, 2], F32, name="prod")
+        nc.vector.tensor_tensor(out=prod[:], in0=num[:], in1=rstd[:], op=ALU.mult)
+        nc.vector.tensor_scalar(
+            out=res[:, 0:2], in0=prod[:], scalar1=cst[:, 1:2], scalar2=0.0, op0=ALU.add, op1=ALU.max
+        )
+        rps = psum.tile([P, P], F32, tag="bank", name="rps")
+        nc.tensor.transpose(rps[:], res[:], ident[:])
+        fin = keep.tile([P, P], F32, name="fin")
+        nc.vector.tensor_copy(out=fin[:], in_=rps[:])
+        nc.sync.dma_start(out=out.rearrange("(m r) o -> m (r o)", m=2), in_=fin[0:2, :])

@@ -26,83 +26,107 @@ K1 = 1.0 / (2 * N)
 K2 = 1.0 / (4 * N)
 FLOPS = 2 * ROWS * K * N
 
-CHUNKS = [(4, 2)] * 7 + [(2, 4), (1, 4), (1, 4)]
+LOAD_TILES = 4
+LOADS = N // (P * LOAD_TILES)
+FIRST_CUT = [1, 1, 2, 2, 2]
+CUT = [2, 2, 2, 2]
+HALF = N // 2
+CHUNKS = [4, 4, 4, 4, 4, 4, 4, 3, 1]
 NC = len(CHUNKS)
-PINNED = True
-LEAD = 4
+LEAD = 6
 
 
 def tile_modelnew_w_kernel(
     tc, x, weight_words, weight_scales, bias, bn_weight, bn_bias, bn_mean, bn_var, gn_weight, gn_bias, out
 ):
     nc = tc.nc
-    assert sum(ch[0] for ch in CHUNKS) * P == N
-    starts = [sum(ch[0] for ch in CHUNKS[:c]) for c in range(NC)]
+    assert sum(CHUNKS) * P == N
+    starts = [sum(CHUNKS[:c]) for c in range(NC)]
     with ExitStack() as ctx:
-        if PINNED:
-            ctx.enter_context(tc.manual_schedule())
+        ctx.enter_context(tc.manual_schedule())
         keep = ctx.enter_context(tc.tile_pool(name="keep", bufs=1))
         work = ctx.enter_context(tc.tile_pool(name="work", bufs=3))
         psum = ctx.enter_context(tc.psum_pool(name="psum", bufs=8))
 
-        planes = keep.tile([P, 2, N], U8, align_bytes=64, name="planes")
-        nc.vector.memset(planes[:].rearrange("p s n -> p (s n)").bitcast(I32), 0)
-        gwrow = keep.tile([P, N], BF16, name="gwrow")
-        nc.vector.memset(gwrow[:].bitcast(I32), 0)
-        vecs = keep.tile([P, 2, P], BF16, name="vecs")
-        nc.vector.memset(vecs[96:128, 1, :], 0.0)
         one = keep.tile([P, 1], F32, name="one")
         nc.vector.memset(one[:], 1.0)
+        eps_t = keep.tile([P, 1], F32, name="eps_t")
+        nc.vector.memset(eps_t[:], EPS)
+        planes = []
+        for h in range(2):
+            pl = keep.tile([P, 2, HALF], U8, align_bytes=64, name="planes%d" % h)
+            planes.append(pl)
+        nc.vector.memset(planes[0][:].rearrange("p s n -> p (s n)").bitcast(I32), 0)
+        gwrow = keep.tile([P, N], BF16, name="gwrow")
+        nc.vector.memset(gwrow[:].bitcast(I32), 0)
+        nc.vector.memset(planes[1][:].rearrange("p s n -> p (s n)").bitcast(I32), 0)
+        vecs = keep.tile([P, 2, P], BF16, name="vecs")
+        nc.vector.memset(vecs[32:64, 1, :], 0.0)
+        nc.vector.memset(vecs[64:128, 1, :], 0.0)
+        gv = keep.tile([P, 2, P], BF16, name="gv")
+        nc.vector.memset(gv[32:64, :, :], 0.0)
+        nc.vector.memset(gv[64:128, :, :], 0.0)
         stv = keep.tile([P, 3, 2, NC], F32, name="stv")
         nc.vector.memset(stv[:], 0.0)
 
         ident = keep.tile([P, P], F32, name="ident")
         make_identity(nc, ident[:])
-
-        xv = x.rearrange("(m p) k -> p m k", p=P)
-        xs = []
-        for q in range(4):
-            xq = keep.tile([P, 2, 1024], BF16, name="x%d" % q)
-            nc.sync.dma_start(out=xq[:], in_=xv[:, :, 1024 * q : 1024 * (q + 1)])
-            xs.append(xq)
-        for i, v in enumerate([bias, bn_weight, bn_bias, bn_mean, bn_var, gn_weight, gn_bias]):
-            r0 = 32 * (i % 4)
-            queue = nc.scalar if i < 4 else nc.gpsimd
-            queue.dma_start(out=vecs[r0 : r0 + 32, i // 4, :], in_=v.rearrange("(j p) -> j p", p=P))
-            if i == 4:
-                nc.gpsimd.dma_start(out=gwrow[0:1, :], in_=gn_weight.rearrange("(o n) -> o n", o=1))
         ones_bf = keep.tile([P, P], BF16, name="ones_bf")
         nc.gpsimd.memset(ones_bf[:], K1)
         ones_n = keep.tile([P, P], F32, name="ones_n")
         nc.gpsimd.memset(ones_n[:], 1.0 / N)
         res = keep.tile([P, P], F32, name="res")
         nc.gpsimd.memset(res[:], 0.0)
-        for s in range(2):
-            for quad in range(4):
-                nc.sync.dma_start(
-                    out=planes[32 * quad : 32 * quad + 16, s, :].bitcast(I32),
-                    in_=weight_scales[4 * s : 4 * s + 4, 4 * quad : 4 * quad + 4, :].bitcast(I32),
-                )
+
+        def by_rows(v):
+            return v.rearrange("(j p) -> j p", p=P)
+
+        for i, v in enumerate([bias, bn_weight, bn_bias, bn_mean, bn_var]):
+            r0 = 32 * (i % 4)
+            nc.sync.dma_start(out=vecs[r0 : r0 + 32, i // 4, :], in_=by_rows(v))
+        xv = x.rearrange("(m p) k -> p m k", p=P)
+        xs = []
+        for q in range(4):
+            xq = keep.tile([P, 2, 1024], BF16, name="x%d" % q)
+            nc.sync.dma_start(out=xq[:], in_=xv[:, :, 1024 * q : 1024 * (q + 1)])
+            xs.append(xq)
+        nc.sync.dma_start(out=gwrow[0:1, :], in_=gn_weight.rearrange("(o n) -> o n", o=1))
+
+        def load_scales(h):
+            for s in range(2):
+                for quad in range(4):
+                    nc.sync.dma_start(
+                        out=planes[h][32 * quad : 32 * quad + 16, s, :].bitcast(I32),
+                        in_=weight_scales[4 * s : 4 * s + 4, 4 * quad : 4 * quad + 4, h * HALF : (h + 1) * HALF].bitcast(I32),
+                    )
+
         wv = weight_words.rearrange("g p n t -> p g (n t)")
-        wtiles = []
-        for c, (tiles, gd) in enumerate(CHUNKS):
-            cols = tiles * P
-            n0 = starts[c] * P
-            pieces = []
-            for d in range(PASSES // gd):
-                wt = keep.tile([P, gd, cols], U32, align_bytes=64, name="w%d_%d" % (c, d))
+        where = {}
+        load_scales(0)
+        for d in range(LOADS):
+            if d * LOAD_TILES * P == HALF:
+                load_scales(1)
+            cols = LOAD_TILES * P
+            n0 = d * cols
+            g0 = 0
+            for i, gd in enumerate(FIRST_CUT if d == 0 else CUT):
+                wt = keep.tile([P, gd, cols], U32, align_bytes=64, name="w%d_%d" % (d, i))
                 nc.sync.dma_start(
-                    out=wt[:].bitcast(I32),
-                    in_=wv[:, d * gd : (d + 1) * gd, 4 * n0 : 4 * (n0 + cols)].bitcast(I32),
+                    out=wt[:].bitcast(I32), in_=wv[:, g0 : g0 + gd, 4 * n0 : 4 * (n0 + cols)].bitcast(I32)
                 )
-                pieces.append(wt)
-            wtiles.append(pieces)
+                for g in range(g0, g0 + gd):
+                    where[(d, g)] = (wt, g - g0)
+                g0 += gd
+            if d == 0:
+                nc.sync.dma_start(out=gv[0:32, 0, :], in_=by_rows(gn_weight))
+                nc.sync.dma_start(out=gv[0:32, 1, :], in_=by_rows(gn_bias))
 
         junk0 = keep.tile([P, 1], F32, name="junk0")
         nc.scalar.activation(out=junk0[:], in_=one[:], func=ACT.Sqrt)
 
         xc = keep.tile([P, PASSES, ROWS], U32, align_bytes=64, name="xc")
         xsc = keep.tile([P, PASSES, ROWS], U8, align_bytes=64, name="xsc")
+        vecf = keep.tile([P, 2, P], F32, name="vecf")
         for g in range(PASSES):
             xt = psum.tile([P, 2, ROWS], F32, tag="bank", name="xt%d" % g)
             for m in range(2):
@@ -116,36 +140,29 @@ def tile_modelnew_w_kernel(
                 in_=xt[:].rearrange("p u r -> p r u"),
             )
             nc.vector.quantize_mx(out=xc[:, g, :].bitcast(FP8X4), scales=xsc[:, g, :], in_=grp[:])
+            if g == 0:
+                nc.vector.tensor_copy(out=vecf[:], in_=vecs[:])
 
-        vecf = keep.tile([P, 2, P], F32, name="vecf")
-        nc.vector.tensor_copy(out=vecf[:], in_=vecs[:])
         vps = psum.tile([P, 2, P], F32, tag="bank", name="vps")
         for h in range(2):
             nc.tensor.transpose(vps[:, h, :], vecf[:, h, :], ident[:])
-        vt = keep.tile([P, 2 * P], F32, name="vt")
-        nc.vector.tensor_copy(out=vt[:], in_=vps[:].rearrange("p h j -> p (h j)"))
-        v_bias, v_bnw, v_bnb, v_bnm = vt[:, 0:32], vt[:, 32:64], vt[:, 64:96], vt[:, 96:128]
-        v_var = vt[:, 128:160]
-        ve = keep.tile([P, 32], F32, name="ve")
-        nc.vector.tensor_scalar_add(out=ve[:], in0=v_var, scalar1=EPS)
+        vt = keep.tile([P, 160], F32, name="vt")
+        nc.vector.tensor_copy(out=vt[:], in_=vps[:].rearrange("p h j -> p (h j)")[:, 0:160])
+        v_bias, v_bnw, v_bnb, v_bnm, v_var = vt[:, 0:32], vt[:, 32:64], vt[:, 64:96], vt[:, 96:128], vt[:, 128:160]
         sd = keep.tile([P, 32], F32, name="sd")
-        nc.scalar.activation(out=sd[:], in_=ve[:], func=ACT.Sqrt)
+        nc.scalar.activation(out=sd[:], in_=v_var, func=ACT.Sqrt, bias=eps_t[:])
         junk1 = keep.tile([P, 1], F32, name="junk1")
         nc.scalar.activation(out=junk1[:], in_=sd[:, 0:1], func=ACT.Tanh)
+        gd0 = keep.tile([P, 32], F32, name="gd0")
+        nc.vector.tensor_tensor(out=gd0[:], in0=v_bias, in1=v_bnm, op=ALU.subtract)
         rs = keep.tile([P, 32], F32, name="rs")
         nc.vector.reciprocal(out=rs[:], in_=sd[:])
         ga = keep.tile([P, 32], F32, name="ga")
         nc.vector.tensor_tensor(out=ga[:], in0=v_bnw, in1=rs[:], op=ALU.mult)
-        gd0 = keep.tile([P, 32], F32, name="gd0")
-        nc.vector.tensor_tensor(out=gd0[:], in0=v_bias, in1=v_bnm, op=ALU.subtract)
         gd1 = keep.tile([P, 32], F32, name="gd1")
         nc.vector.tensor_tensor(out=gd1[:], in0=gd0[:], in1=ga[:], op=ALU.mult)
         gb = keep.tile([P, 32], F32, name="gb")
         nc.vector.tensor_tensor(out=gb[:], in0=gd1[:], in1=v_bnb, op=ALU.add)
-        gsum = keep.tile([P, 2], F32, name="gsum")
-        nc.vector.tensor_reduce(
-            out=gsum[:], in_=vt[:, 160:224].rearrange("p (v j) -> p v j", v=2), axis=AX.X, op=ALU.add
-        )
 
         gwbc = keep.tile([P, N], BF16, name="gwbc")
         for h in range(4):
@@ -156,42 +173,40 @@ def tile_modelnew_w_kernel(
                     out=gps[:, i * 512 : (i + 1) * 512], lhsT=ones_bf[:], rhs=gwrow[:, lo : lo + 512], start=True, stop=True
                 )
             nc.scalar.copy(out=gwbc[:, h * 1024 : (h + 1) * 1024], in_=gps[:])
-        cps = psum.tile([P, 2], F32, tag="bank", name="cps")
-        nc.tensor.matmul(out=cps[:], lhsT=ones_n[:], rhs=gsum[:], start=True, stop=True)
-        cst = keep.tile([P, 2], F32, name="cst")
-        nc.vector.tensor_scalar(out=cst[:, 0:1], in0=cps[:, 0:1], scalar1=-K1, scalar2=None, op0=ALU.mult)
-        nc.vector.tensor_copy(out=cst[:, 1:2], in_=cps[:, 1:2])
 
         st2 = keep.tile([P, 2, NC - 1], F32, name="st2")
         junk_s = keep.tile([P, 512], F32, name="junk_s")
         junk_v = keep.tile([P, 512], F32, name="junk_v")
+        gsum = keep.tile([P, 2], F32, name="gsum")
+        cst = keep.tile([P, 2], F32, name="cst")
         mx = {}
         zs = {}
         zts = {}
         es = {}
 
         def pass_order(c):
-            tiles = CHUNKS[c][0]
+            tiles = CHUNKS[c]
             early = [(g, t) for g in range(PASSES - 2) for t in range(tiles)]
             late = [(g, t) for t in range(tiles) for g in (PASSES - 2, PASSES - 1)]
             return early + late
 
         def passes(c, todo):
-            tiles, gd = CHUNKS[c]
             if c not in mx:
                 banks = []
-                for t in range(tiles):
+                for t in range(CHUNKS[c]):
                     bank = psum.tile([P, ROWS], F32, tag="bank", name="mx%d_%d" % (c, t))
                     banks.append(bank)
                 mx[c] = banks
             for g, t in todo:
-                wt = wtiles[c][g // gd]
+                j = starts[c] + t
+                wt, gi = where[(j // LOAD_TILES, g)]
+                lo = (j % LOAD_TILES) * P
                 s, kk = divmod(g, 4)
-                n0 = (starts[c] + t) * P
+                n0 = (j * P) % HALF
                 nc.tensor.matmul_mx(
                     out=mx[c][t][:],
-                    lhsT=wt[:, g % gd, t * P : (t + 1) * P].bitcast(FP8X4),
-                    lhsT_scale=planes[4 * kk : P, s, n0 : n0 + P],
+                    lhsT=wt[:, gi, lo : lo + P].bitcast(FP8X4),
+                    lhsT_scale=planes[(j * P) // HALF][4 * kk : P, s, n0 : n0 + P],
                     rhs=xc[:, g, :].bitcast(FP8X4),
                     rhs_scale=xsc[:, g, :],
                     start=(g == 0),
@@ -199,9 +214,8 @@ def tile_modelnew_w_kernel(
                 )
 
         def evac(c):
-            tiles = CHUNKS[c][0]
             zl = []
-            for t in range(tiles):
+            for t in range(CHUNKS[c]):
                 j = starts[c] + t
                 z = work.tile([P, ROWS], F32, tag="z", bufs=8, name="z%d" % j)
                 if t % 2 == 0:
@@ -217,17 +231,16 @@ def tile_modelnew_w_kernel(
             zs[c] = zl
 
         def transposes(c):
-            tiles = CHUNKS[c][0]
             zl = []
             for m in range(2):
                 zt = psum.tile([P, 512], F32, tag="bank", name="zt%d_%d" % (c, m))
-                for t in range(tiles):
+                for t in range(CHUNKS[c]):
                     nc.tensor.transpose(zt[:, t * P : (t + 1) * P], zs[c][t][:, m * P : (m + 1) * P], ident[:])
                 zl.append(zt)
             zts[c] = zl
 
         def mainops(c):
-            w = CHUNKS[c][0] * P
+            w = CHUNKS[c] * P
             el = []
             for m in range(2):
                 e = work.tile([P, 512], F32, tag="e", bufs=6, name="e%d_%d" % (c, m))
@@ -247,7 +260,7 @@ def tile_modelnew_w_kernel(
                 )
 
         def tailops(c):
-            w = CHUNKS[c][0] * P
+            w = CHUNKS[c] * P
             n0 = starts[c] * P
             for m in range(2):
                 e = es[c][m]
@@ -269,9 +282,16 @@ def tile_modelnew_w_kernel(
             if c + 1 < NC:
                 passes(c + 1, pass_order(c + 1)[:LEAD])
             transposes(c)
+            if c == 1:
+                nc.vector.tensor_reduce(out=gsum[:], in_=gv[:], axis=AX.X, op=ALU.add)
+                cps = psum.tile([P, 2], F32, tag="bank", name="cps")
+                nc.tensor.matmul(out=cps[:], lhsT=ones_n[:], rhs=gsum[:], start=True, stop=True)
             if c >= 1:
                 tailops(c - 1)
             mainops(c)
+            if c == 1:
+                nc.vector.tensor_scalar(out=cst[:, 0:1], in0=cps[:, 0:1], scalar1=-K1, scalar2=None, op0=ALU.mult)
+                nc.vector.tensor_copy(out=cst[:, 1:2], in_=cps[:, 1:2])
             if c + 1 < NC:
                 passes(c + 1, pass_order(c + 1)[LEAD:])
         junk2 = keep.tile([P, 1], F32, name="junk2")
@@ -282,14 +302,12 @@ def tile_modelnew_w_kernel(
         r = keep.tile([P, 6], F32, name="r")
         nc.vector.tensor_reduce(out=r[:], in_=stv[:].rearrange("p w m c -> p (w m) c"), axis=AX.X, op=ALU.add)
         s1, s3, s2 = r[:, 0:2], r[:, 2:4], r[:, 4:6]
-        t2 = keep.tile([P, 2], F32, name="t2")
-        nc.vector.tensor_scalar(out=t2[:], in0=s2, scalar1=K2, scalar2=EPS, op0=ALU.mult, op1=ALU.add)
         msq = keep.tile([P, 2], F32, name="msq")
-        nc.vector.scalar_tensor_tensor(out=msq[:], in0=s1, scalar=K1 * K1, in1=s1, op0=ALU.mult, op1=ALU.mult)
+        nc.vector.scalar_tensor_tensor(out=msq[:], in0=s1, scalar=-K1 * K1, in1=s1, op0=ALU.mult, op1=ALU.mult)
         var = keep.tile([P, 2], F32, name="var")
-        nc.vector.tensor_tensor(out=var[:], in0=t2[:], in1=msq[:], op=ALU.subtract)
+        nc.vector.scalar_tensor_tensor(out=var[:], in0=s2, scalar=K2, in1=msq[:], op0=ALU.mult, op1=ALU.add)
         sd2 = keep.tile([P, 2], F32, name="sd2")
-        nc.scalar.activation(out=sd2[:], in_=var[:], func=ACT.Sqrt)
+        nc.scalar.activation(out=sd2[:], in_=var[:], func=ACT.Sqrt, bias=eps_t[:])
         num = keep.tile([P, 2], F32, name="num")
         nc.vector.scalar_tensor_tensor(out=num[:], in0=s1, scalar=cst[:, 0:1], in1=s3, op0=ALU.mult, op1=ALU.add)
         rstd = keep.tile([P, 2], F32, name="rstd")

@@ -31,7 +31,7 @@ LOADS = N // (P * LOAD_TILES)
 FIRST_CUT = [1, 1, 2, 2, 2]
 CUT = [2, 2, 2, 2]
 HALF = N // 2
-CHUNKS = [4, 4, 4, 4, 4, 4, 4, 3, 1]
+CHUNKS = [4, 4, 4, 4, 4, 4, 3, 3, 2]
 NC = len(CHUNKS)
 LEAD = 6
 
@@ -239,65 +239,86 @@ def tile_modelnew_w_kernel(
                 zl.append(zt)
             zts[c] = zl
 
-        def mainops(c):
+        def squares(c):
             w = CHUNKS[c] * P
-            el = []
+            e = work.tile([P, 2, 512], F32, tag="e", bufs=4, name="e%d" % c)
+            es[c] = e
             for m in range(2):
-                e = work.tile([P, 512], F32, tag="e", bufs=6, name="e%d_%d" % (c, m))
-                nc.scalar.activation(out=e[:, :w], in_=zts[c][m][:, :w], func=ACT.Square)
-                el.append(e)
-            es[c] = el
+                nc.scalar.activation(out=e[:, m, :w], in_=zts[c][m][:, :w], func=ACT.Square)
+
+        def cubes(c):
+            w = CHUNKS[c] * P
             for m in range(2):
+                e = es[c][:, m, :w]
+                nc.vector.scalar_tensor_tensor(out=e, in0=e, scalar=KAPPA, in1=zts[c][m][:, :w], op0=ALU.add, op1=ALU.mult)
+
+        def tanhs(c):
+            w = CHUNKS[c] * P
+            nc.scalar.activation(out=es[c][:, :, :w], in_=es[c][:, :, :w], func=ACT.Tanh, scale=C2)
+
+        def gelus(c):
+            w = CHUNKS[c] * P
+            for m in range(2):
+                e = es[c][:, m, :w]
                 nc.vector.scalar_tensor_tensor(
-                    out=el[m][:, :w], in0=el[m][:, :w], scalar=KAPPA, in1=zts[c][m][:, :w], op0=ALU.add, op1=ALU.mult
-                )
-            for m in range(2):
-                nc.scalar.activation(out=el[m][:, :w], in_=el[m][:, :w], func=ACT.Tanh, scale=C2)
-            for m in range(2):
-                nc.vector.scalar_tensor_tensor(
-                    out=el[m][:, :w], in0=el[m][:, :w], scalar=1.0, in1=zts[c][m][:, :w], op0=ALU.add, op1=ALU.mult,
+                    out=e, in0=e, scalar=1.0, in1=zts[c][m][:, :w], op0=ALU.add, op1=ALU.mult,
                     accum_out=stv[:, 0, m, c : c + 1],
                 )
 
-        def tailops(c):
+        def square_sums(c):
+            w = CHUNKS[c] * P
+            for m in range(2):
+                e = es[c][:, m, :w]
+                if c < NC - 1:
+                    nc.scalar.activation(out=junk_s[:, :w], in_=e, func=ACT.Square, accum_out=st2[:, m, c : c + 1])
+                else:
+                    nc.vector.scalar_tensor_tensor(
+                        out=junk_v[:, :w], in0=e, scalar=1.0, in1=e, op0=ALU.mult, op1=ALU.mult,
+                        accum_out=stv[:, 2, m, c : c + 1],
+                    )
+
+        def weighted_sums(c):
             w = CHUNKS[c] * P
             n0 = starts[c] * P
             for m in range(2):
-                e = es[c][m]
-                if c < NC - 1:
-                    nc.scalar.activation(out=junk_s[:, :w], in_=e[:, :w], func=ACT.Square, accum_out=st2[:, m, c : c + 1])
-                else:
-                    nc.vector.scalar_tensor_tensor(
-                        out=junk_v[:, :w], in0=e[:, :w], scalar=1.0, in1=e[:, :w], op0=ALU.mult, op1=ALU.mult,
-                        accum_out=stv[:, 2, m, c : c + 1],
-                    )
                 nc.vector.scalar_tensor_tensor(
-                    out=junk_v[:, :w], in0=e[:, :w], scalar=1.0, in1=gwbc[:, n0 : n0 + w], op0=ALU.mult, op1=ALU.mult,
+                    out=junk_v[:, :w], in0=es[c][:, m, :w], scalar=1.0, in1=gwbc[:, n0 : n0 + w], op0=ALU.mult, op1=ALU.mult,
                     accum_out=stv[:, 1, m, c : c + 1],
                 )
 
+        junk2 = keep.tile([P, 1], F32, name="junk2")
         passes(0, pass_order(0))
-        for c in range(NC):
-            evac(c)
-            if c + 1 < NC:
-                passes(c + 1, pass_order(c + 1)[:LEAD])
-            transposes(c)
-            if c == 1:
+        for rnd in range(1, NC + 3):
+            c1, c2, c3 = rnd - 1, rnd - 2, rnd - 3
+            if c1 < NC:
+                evac(c1)
+            if rnd < NC:
+                passes(rnd, pass_order(rnd)[:LEAD])
+            if c1 < NC:
+                transposes(c1)
+            if c1 == 1:
                 nc.vector.tensor_reduce(out=gsum[:], in_=gv[:], axis=AX.X, op=ALU.add)
                 cps = psum.tile([P, 2], F32, tag="bank", name="cps")
                 nc.tensor.matmul(out=cps[:], lhsT=ones_n[:], rhs=gsum[:], start=True, stop=True)
-            if c >= 1:
-                tailops(c - 1)
-            mainops(c)
-            if c == 1:
+            if 0 <= c2 < NC:
+                tanhs(c2)
+            if c2 == NC - 1:
+                nc.scalar.activation(out=junk2[:], in_=one[:], func=ACT.Sqrt)
+                nc.vector.tensor_reduce(out=stv[:, 2, :, 0], in_=st2[:], axis=AX.X, op=ALU.add)
+            if 0 <= c3 < NC:
+                weighted_sums(c3)
+            if 0 <= c2 < NC:
+                gelus(c2)
+            if c1 < NC:
+                squares(c1)
+                cubes(c1)
+            if 0 <= c2 < NC:
+                square_sums(c2)
+            if c1 == 1:
                 nc.vector.tensor_scalar(out=cst[:, 0:1], in0=cps[:, 0:1], scalar1=-K1, scalar2=None, op0=ALU.mult)
                 nc.vector.tensor_copy(out=cst[:, 1:2], in_=cps[:, 1:2])
-            if c + 1 < NC:
-                passes(c + 1, pass_order(c + 1)[LEAD:])
-        junk2 = keep.tile([P, 1], F32, name="junk2")
-        nc.scalar.activation(out=junk2[:], in_=one[:], func=ACT.Sqrt)
-        nc.vector.tensor_reduce(out=stv[:, 2, :, 0], in_=st2[:], axis=AX.X, op=ALU.add)
-        tailops(NC - 1)
+            if rnd < NC:
+                passes(rnd, pass_order(rnd)[LEAD:])
 
         r = keep.tile([P, 6], F32, name="r")
         nc.vector.tensor_reduce(out=r[:], in_=stv[:].rearrange("p w m c -> p (w m) c"), axis=AX.X, op=ALU.add)

@@ -31,8 +31,9 @@ LOADS = N // (P * LOAD_TILES)
 FIRST_CUT = [1, 1, 2, 2, 2]
 CUT = [2, 2, 2, 2]
 HALF = N // 2
-CHUNKS = [4, 4, 4, 4, 4, 4, 3, 3, 2]
+CHUNKS = [4, 4, 4, 4, 4, 4, 4, 3, 1]
 NC = len(CHUNKS)
+WARM = 8
 LEAD = 6
 
 
@@ -56,9 +57,9 @@ def tile_modelnew_w_kernel(
         for h in range(2):
             pl = keep.tile([P, 2, HALF], U8, align_bytes=64, name="planes%d" % h)
             planes.append(pl)
-        nc.vector.memset(planes[0][:].rearrange("p s n -> p (s n)").bitcast(I32), 0)
         gwrow = keep.tile([P, N], BF16, name="gwrow")
         nc.vector.memset(gwrow[:].bitcast(I32), 0)
+        nc.vector.memset(planes[0][:].rearrange("p s n -> p (s n)").bitcast(I32), 0)
         nc.vector.memset(planes[1][:].rearrange("p s n -> p (s n)").bitcast(I32), 0)
         vecs = keep.tile([P, 2, P], BF16, name="vecs")
         nc.vector.memset(vecs[32:64, 1, :], 0.0)
@@ -69,10 +70,12 @@ def tile_modelnew_w_kernel(
         stv = keep.tile([P, 3, 2, NC], F32, name="stv")
         nc.vector.memset(stv[:], 0.0)
 
-        ident = keep.tile([P, P], F32, name="ident")
-        make_identity(nc, ident[:])
         ones_bf = keep.tile([P, P], BF16, name="ones_bf")
         nc.gpsimd.memset(ones_bf[:], K1)
+        warm = keep.tile([P, 512], BF16, name="warm")
+        nc.gpsimd.memset(warm[:], 0.0)
+        ident = keep.tile([P, P], F32, name="ident")
+        make_identity(nc, ident[:])
         ones_n = keep.tile([P, P], F32, name="ones_n")
         nc.gpsimd.memset(ones_n[:], 1.0 / N)
         res = keep.tile([P, P], F32, name="res")
@@ -90,7 +93,8 @@ def tile_modelnew_w_kernel(
             xq = keep.tile([P, 2, 1024], BF16, name="x%d" % q)
             nc.sync.dma_start(out=xq[:], in_=xv[:, :, 1024 * q : 1024 * (q + 1)])
             xs.append(xq)
-        nc.sync.dma_start(out=gwrow[0:1, :], in_=gn_weight.rearrange("(o n) -> o n", o=1))
+            if q == 0:
+                nc.sync.dma_start(out=gwrow[0:1, :], in_=gn_weight.rearrange("(o n) -> o n", o=1))
 
         def load_scales(h):
             for s in range(2):
@@ -127,6 +131,24 @@ def tile_modelnew_w_kernel(
         xc = keep.tile([P, PASSES, ROWS], U32, align_bytes=64, name="xc")
         xsc = keep.tile([P, PASSES, ROWS], U8, align_bytes=64, name="xsc")
         vecf = keep.tile([P, 2, P], F32, name="vecf")
+        gwbc = keep.tile([P, N], BF16, name="gwbc")
+        idle = psum.tile([P, 512], F32, tag="bank", name="idle")
+        for i in range(WARM):
+            nc.tensor.matmul(out=idle[:], lhsT=ones_bf[:], rhs=warm[:], start=True, stop=True)
+        gpss = []
+
+        def spread(i):
+            if i % 2 == 0:
+                gps = psum.tile([P, 1024], BF16, tag="bank", name="gps%d" % (i // 2))
+                gpss.append(gps)
+            half = (i % 2) * 512
+            nc.tensor.matmul(
+                out=gpss[i // 2][:, half : half + 512], lhsT=ones_bf[:], rhs=gwrow[:, i * 512 : (i + 1) * 512],
+                start=True, stop=True,
+            )
+            if i % 2 == 1:
+                nc.vector.tensor_copy(out=gwbc[:, (i - 1) * 512 : (i + 1) * 512], in_=gpss[i // 2][:])
+
         for g in range(PASSES):
             xt = psum.tile([P, 2, ROWS], F32, tag="bank", name="xt%d" % g)
             for m in range(2):
@@ -142,6 +164,10 @@ def tile_modelnew_w_kernel(
             nc.vector.quantize_mx(out=xc[:, g, :].bitcast(FP8X4), scales=xsc[:, g, :], in_=grp[:])
             if g == 0:
                 nc.vector.tensor_copy(out=vecf[:], in_=vecs[:])
+                nc.tensor.matmul(out=idle[:], lhsT=ones_bf[:], rhs=warm[:], start=True, stop=True)
+            else:
+                spread(g - 1)
+        spread(PASSES - 1)
 
         vps = psum.tile([P, 2, P], F32, tag="bank", name="vps")
         for h in range(2):
@@ -163,16 +189,6 @@ def tile_modelnew_w_kernel(
         nc.vector.tensor_tensor(out=gd1[:], in0=gd0[:], in1=ga[:], op=ALU.mult)
         gb = keep.tile([P, 32], F32, name="gb")
         nc.vector.tensor_tensor(out=gb[:], in0=gd1[:], in1=v_bnb, op=ALU.add)
-
-        gwbc = keep.tile([P, N], BF16, name="gwbc")
-        for h in range(4):
-            gps = psum.tile([P, 1024], BF16, tag="bank", name="gps%d" % h)
-            for i in range(2):
-                lo = (2 * h + i) * 512
-                nc.tensor.matmul(
-                    out=gps[:, i * 512 : (i + 1) * 512], lhsT=ones_bf[:], rhs=gwrow[:, lo : lo + 512], start=True, stop=True
-                )
-            nc.scalar.copy(out=gwbc[:, h * 1024 : (h + 1) * 1024], in_=gps[:])
 
         st2 = keep.tile([P, 2, NC - 1], F32, name="st2")
         junk_s = keep.tile([P, 512], F32, name="junk_s")
@@ -239,86 +255,65 @@ def tile_modelnew_w_kernel(
                 zl.append(zt)
             zts[c] = zl
 
-        def squares(c):
+        def mainops(c):
             w = CHUNKS[c] * P
-            e = work.tile([P, 2, 512], F32, tag="e", bufs=4, name="e%d" % c)
-            es[c] = e
+            el = []
             for m in range(2):
-                nc.scalar.activation(out=e[:, m, :w], in_=zts[c][m][:, :w], func=ACT.Square)
-
-        def cubes(c):
-            w = CHUNKS[c] * P
+                e = work.tile([P, 512], F32, tag="e", bufs=6, name="e%d_%d" % (c, m))
+                nc.scalar.activation(out=e[:, :w], in_=zts[c][m][:, :w], func=ACT.Square)
+                el.append(e)
+            es[c] = el
             for m in range(2):
-                e = es[c][:, m, :w]
-                nc.vector.scalar_tensor_tensor(out=e, in0=e, scalar=KAPPA, in1=zts[c][m][:, :w], op0=ALU.add, op1=ALU.mult)
-
-        def tanhs(c):
-            w = CHUNKS[c] * P
-            nc.scalar.activation(out=es[c][:, :, :w], in_=es[c][:, :, :w], func=ACT.Tanh, scale=C2)
-
-        def gelus(c):
-            w = CHUNKS[c] * P
-            for m in range(2):
-                e = es[c][:, m, :w]
                 nc.vector.scalar_tensor_tensor(
-                    out=e, in0=e, scalar=1.0, in1=zts[c][m][:, :w], op0=ALU.add, op1=ALU.mult,
+                    out=el[m][:, :w], in0=el[m][:, :w], scalar=KAPPA, in1=zts[c][m][:, :w], op0=ALU.add, op1=ALU.mult
+                )
+            for m in range(2):
+                nc.scalar.activation(out=el[m][:, :w], in_=el[m][:, :w], func=ACT.Tanh, scale=C2)
+            for m in range(2):
+                nc.vector.scalar_tensor_tensor(
+                    out=el[m][:, :w], in0=el[m][:, :w], scalar=1.0, in1=zts[c][m][:, :w], op0=ALU.add, op1=ALU.mult,
                     accum_out=stv[:, 0, m, c : c + 1],
                 )
 
-        def square_sums(c):
-            w = CHUNKS[c] * P
-            for m in range(2):
-                e = es[c][:, m, :w]
-                if c < NC - 1:
-                    nc.scalar.activation(out=junk_s[:, :w], in_=e, func=ACT.Square, accum_out=st2[:, m, c : c + 1])
-                else:
-                    nc.vector.scalar_tensor_tensor(
-                        out=junk_v[:, :w], in0=e, scalar=1.0, in1=e, op0=ALU.mult, op1=ALU.mult,
-                        accum_out=stv[:, 2, m, c : c + 1],
-                    )
-
-        def weighted_sums(c):
+        def tailops(c):
             w = CHUNKS[c] * P
             n0 = starts[c] * P
             for m in range(2):
+                e = es[c][m]
+                if c < NC - 1:
+                    nc.scalar.activation(out=junk_s[:, :w], in_=e[:, :w], func=ACT.Square, accum_out=st2[:, m, c : c + 1])
+                else:
+                    nc.vector.scalar_tensor_tensor(
+                        out=junk_v[:, :w], in0=e[:, :w], scalar=1.0, in1=e[:, :w], op0=ALU.mult, op1=ALU.mult,
+                        accum_out=stv[:, 2, m, c : c + 1],
+                    )
                 nc.vector.scalar_tensor_tensor(
-                    out=junk_v[:, :w], in0=es[c][:, m, :w], scalar=1.0, in1=gwbc[:, n0 : n0 + w], op0=ALU.mult, op1=ALU.mult,
+                    out=junk_v[:, :w], in0=e[:, :w], scalar=1.0, in1=gwbc[:, n0 : n0 + w], op0=ALU.mult, op1=ALU.mult,
                     accum_out=stv[:, 1, m, c : c + 1],
                 )
 
-        junk2 = keep.tile([P, 1], F32, name="junk2")
         passes(0, pass_order(0))
-        for rnd in range(1, NC + 3):
-            c1, c2, c3 = rnd - 1, rnd - 2, rnd - 3
-            if c1 < NC:
-                evac(c1)
-            if rnd < NC:
-                passes(rnd, pass_order(rnd)[:LEAD])
-            if c1 < NC:
-                transposes(c1)
-            if c1 == 1:
+        for c in range(NC):
+            evac(c)
+            if c + 1 < NC:
+                passes(c + 1, pass_order(c + 1)[:LEAD])
+            transposes(c)
+            if c == 1:
                 nc.vector.tensor_reduce(out=gsum[:], in_=gv[:], axis=AX.X, op=ALU.add)
                 cps = psum.tile([P, 2], F32, tag="bank", name="cps")
                 nc.tensor.matmul(out=cps[:], lhsT=ones_n[:], rhs=gsum[:], start=True, stop=True)
-            if 0 <= c2 < NC:
-                tanhs(c2)
-            if c2 == NC - 1:
-                nc.scalar.activation(out=junk2[:], in_=one[:], func=ACT.Sqrt)
-                nc.vector.tensor_reduce(out=stv[:, 2, :, 0], in_=st2[:], axis=AX.X, op=ALU.add)
-            if 0 <= c3 < NC:
-                weighted_sums(c3)
-            if 0 <= c2 < NC:
-                gelus(c2)
-            if c1 < NC:
-                squares(c1)
-                cubes(c1)
-            if 0 <= c2 < NC:
-                square_sums(c2)
-            if c1 == 1:
+            if c >= 1:
+                tailops(c - 1)
+            mainops(c)
+            if c == 1:
                 nc.vector.tensor_scalar(out=cst[:, 0:1], in0=cps[:, 0:1], scalar1=-K1, scalar2=None, op0=ALU.mult)
                 nc.vector.tensor_copy(out=cst[:, 1:2], in_=cps[:, 1:2])
-            if rnd < NC:
-                passes(rnd, pass_order(rnd)[LEAD:])
+            if c + 1 < NC:
+                passes(c + 1, pass_order(c + 1)[LEAD:])
+        junk2 = keep.tile([P, 1], F32, name="junk2")
+        nc.scalar.activation(out=junk2[:], in_=one[:], func=ACT.Sqrt)
+        nc.vector.tensor_reduce(out=stv[:, 2, :, 0], in_=st2[:], axis=AX.X, op=ALU.add)
+        tailops(NC - 1)
 
         r = keep.tile([P, 6], F32, name="r")
         nc.vector.tensor_reduce(out=r[:], in_=stv[:].rearrange("p w m c -> p (w m) c"), axis=AX.X, op=ALU.add)

@@ -67,8 +67,9 @@ def tile_modelnew_w_kernel(
         gv = keep.tile([P, 2, P], BF16, name="gv")
         nc.vector.memset(gv[32:64, :, :], 0.0)
         nc.vector.memset(gv[64:128, :, :], 0.0)
-        stv = keep.tile([P, 3, 2, NC], F32, name="stv")
+        stv = keep.tile([P, 3, 2, NC + 1], F32, name="stv")
         nc.vector.memset(stv[:], 0.0)
+        nc.vector.memset(stv[:, 2, :, NC : NC + 1], EPS / K2)
 
         ones_bf = keep.tile([P, P], BF16, name="ones_bf")
         nc.gpsimd.memset(ones_bf[:], K1)
@@ -80,6 +81,8 @@ def tile_modelnew_w_kernel(
         nc.gpsimd.memset(ones_n[:], 1.0 / N)
         res = keep.tile([P, P], F32, name="res")
         nc.gpsimd.memset(res[:], 0.0)
+        nhalf = keep.tile([P, 2], F32, name="nhalf")
+        nc.gpsimd.memset(nhalf[:], -0.5)
 
         def by_rows(v):
             return v.rearrange("(j p) -> j p", p=P)
@@ -190,7 +193,6 @@ def tile_modelnew_w_kernel(
         gb = keep.tile([P, 32], F32, name="gb")
         nc.vector.tensor_tensor(out=gb[:], in0=gd1[:], in1=v_bnb, op=ALU.add)
 
-        st2 = keep.tile([P, 2, NC - 1], F32, name="st2")
         junk_s = keep.tile([P, 512], F32, name="junk_s")
         junk_v = keep.tile([P, 512], F32, name="junk_v")
         gsum = keep.tile([P, 2], F32, name="gsum")
@@ -229,74 +231,89 @@ def tile_modelnew_w_kernel(
                     stop=(g == PASSES - 1),
                 )
 
+        def ev(c, t, on_scalar):
+            j = starts[c] + t
+            z = work.tile([P, ROWS], F32, tag="z", bufs=8, name="z%d" % j)
+            if on_scalar:
+                nc.scalar.activation(
+                    out=z[:], in_=mx[c][t][:], func=ACT.Identity, bias=gb[:, j : j + 1], scale=ga[:, j : j + 1]
+                )
+            else:
+                nc.vector.tensor_scalar(
+                    out=z[:], in0=mx[c][t][:], scalar1=ga[:, j : j + 1], scalar2=gb[:, j : j + 1],
+                    op0=ALU.mult, op1=ALU.add,
+                )
+            zs.setdefault(c, []).append(z)
+
         def evac(c):
-            zl = []
             for t in range(CHUNKS[c]):
-                j = starts[c] + t
-                z = work.tile([P, ROWS], F32, tag="z", bufs=8, name="z%d" % j)
-                if t % 2 == 0:
-                    nc.scalar.activation(
-                        out=z[:], in_=mx[c][t][:], func=ACT.Identity, bias=gb[:, j : j + 1], scale=ga[:, j : j + 1]
-                    )
-                else:
-                    nc.vector.tensor_scalar(
-                        out=z[:], in0=mx[c][t][:], scalar1=ga[:, j : j + 1], scalar2=gb[:, j : j + 1],
-                        op0=ALU.mult, op1=ALU.add,
-                    )
-                zl.append(z)
-            zs[c] = zl
+                ev(c, t, t % 2 == 0)
+
+        def joint(c):
+            return 2 * CHUNKS[c] * P <= 512
 
         def transposes(c):
-            zl = []
-            for m in range(2):
-                zt = psum.tile([P, 512], F32, tag="bank", name="zt%d_%d" % (c, m))
-                for t in range(CHUNKS[c]):
-                    nc.tensor.transpose(zt[:, t * P : (t + 1) * P], zs[c][t][:, m * P : (m + 1) * P], ident[:])
-                zl.append(zt)
-            zts[c] = zl
-
-        def mainops(c):
             w = CHUNKS[c] * P
-            el = []
+            if joint(c):
+                zt = psum.tile([P, 512], F32, tag="bank", name="zt%d" % c)
+                e = work.tile([P, 512], F32, tag="e", bufs=6, name="e%d" % c)
+                zts[c] = [zt[:, m * w : (m + 1) * w] for m in range(2)] + [zt[:, : 2 * w]]
+                es[c] = [e[:, m * w : (m + 1) * w] for m in range(2)] + [e[:, : 2 * w]]
+            else:
+                zts[c] = []
+                es[c] = []
+                for m in range(2):
+                    zt = psum.tile([P, 512], F32, tag="bank", name="zt%d_%d" % (c, m))
+                    e = work.tile([P, 512], F32, tag="e", bufs=6, name="e%d_%d" % (c, m))
+                    zts[c].append(zt[:, :w])
+                    es[c].append(e[:, :w])
             for m in range(2):
-                e = work.tile([P, 512], F32, tag="e", bufs=6, name="e%d_%d" % (c, m))
-                nc.scalar.activation(out=e[:, :w], in_=zts[c][m][:, :w], func=ACT.Square)
-                el.append(e)
-            es[c] = el
-            for m in range(2):
-                nc.vector.scalar_tensor_tensor(
-                    out=el[m][:, :w], in0=el[m][:, :w], scalar=KAPPA, in1=zts[c][m][:, :w], op0=ALU.add, op1=ALU.mult
-                )
-            for m in range(2):
-                nc.scalar.activation(out=el[m][:, :w], in_=el[m][:, :w], func=ACT.Tanh, scale=C2)
-            for m in range(2):
-                nc.vector.scalar_tensor_tensor(
-                    out=el[m][:, :w], in0=el[m][:, :w], scalar=1.0, in1=zts[c][m][:, :w], op0=ALU.add, op1=ALU.mult,
-                    accum_out=stv[:, 0, m, c : c + 1],
-                )
+                for t in range(CHUNKS[c]):
+                    nc.tensor.transpose(zts[c][m][:, t * P : (t + 1) * P], zs[c][t][:, m * P : (m + 1) * P], ident[:])
 
-        def tailops(c):
+        def sq(c, m):
+            nc.scalar.activation(out=es[c][m], in_=zts[c][m], func=ACT.Square)
+
+        def m1(c, m):
+            nc.vector.scalar_tensor_tensor(
+                out=es[c][m], in0=es[c][m], scalar=KAPPA, in1=zts[c][m], op0=ALU.add, op1=ALU.mult
+            )
+
+        def th(c, m):
+            nc.scalar.activation(out=es[c][m], in_=es[c][m], func=ACT.Tanh, scale=C2)
+
+        def m2(c, m):
+            nc.vector.scalar_tensor_tensor(
+                out=es[c][m], in0=es[c][m], scalar=1.0, in1=zts[c][m], op0=ALU.add, op1=ALU.mult,
+                accum_out=stv[:, 0, m, c : c + 1],
+            )
+
+        def s2(c, m):
+            w = CHUNKS[c] * P
+            nc.scalar.activation(out=junk_s[:, :w], in_=es[c][m], func=ACT.Square, accum_out=stv[:, 2, m, c : c + 1])
+
+        def s3(c, m):
             w = CHUNKS[c] * P
             n0 = starts[c] * P
+            nc.vector.scalar_tensor_tensor(
+                out=junk_v[:, :w], in0=es[c][m], scalar=1.0, in1=gwbc[:, n0 : n0 + w], op0=ALU.mult, op1=ALU.mult,
+                accum_out=stv[:, 1, m, c : c + 1],
+            )
+
+        def mainops(c):
+            for step in (sq, m1, th, m2):
+                for m in range(2):
+                    step(c, m)
+
+        def tailops(c):
             for m in range(2):
-                e = es[c][m]
-                if c < NC - 1:
-                    nc.scalar.activation(out=junk_s[:, :w], in_=e[:, :w], func=ACT.Square, accum_out=st2[:, m, c : c + 1])
-                else:
-                    nc.vector.scalar_tensor_tensor(
-                        out=junk_v[:, :w], in0=e[:, :w], scalar=1.0, in1=e[:, :w], op0=ALU.mult, op1=ALU.mult,
-                        accum_out=stv[:, 2, m, c : c + 1],
-                    )
-                nc.vector.scalar_tensor_tensor(
-                    out=junk_v[:, :w], in0=e[:, :w], scalar=1.0, in1=gwbc[:, n0 : n0 + w], op0=ALU.mult, op1=ALU.mult,
-                    accum_out=stv[:, 1, m, c : c + 1],
-                )
+                s2(c, m)
+                s3(c, m)
 
         passes(0, pass_order(0))
-        for c in range(NC):
+        for c in range(NC - 2):
             evac(c)
-            if c + 1 < NC:
-                passes(c + 1, pass_order(c + 1)[:LEAD])
+            passes(c + 1, pass_order(c + 1)[:LEAD])
             transposes(c)
             if c == 1:
                 nc.vector.tensor_reduce(out=gsum[:], in_=gv[:], axis=AX.X, op=ALU.add)
@@ -308,33 +325,48 @@ def tile_modelnew_w_kernel(
             if c == 1:
                 nc.vector.tensor_scalar(out=cst[:, 0:1], in0=cps[:, 0:1], scalar1=-K1, scalar2=None, op0=ALU.mult)
                 nc.vector.tensor_copy(out=cst[:, 1:2], in_=cps[:, 1:2])
-            if c + 1 < NC:
-                passes(c + 1, pass_order(c + 1)[LEAD:])
-        junk2 = keep.tile([P, 1], F32, name="junk2")
-        nc.scalar.activation(out=junk2[:], in_=one[:], func=ACT.Sqrt)
-        nc.vector.tensor_reduce(out=stv[:, 2, :, 0], in_=st2[:], axis=AX.X, op=ALU.add)
-        tailops(NC - 1)
+            passes(c + 1, pass_order(c + 1)[LEAD:])
+
+        a, b = NC - 2, NC - 1
+        assert joint(b) and CHUNKS[b] == 1
+        evac(a)
+        passes(b, pass_order(b)[:LEAD])
+        transposes(a)
+        passes(b, pass_order(b)[LEAD:])
+        tailops(a - 1)
+        sq(a, 0)
+        sq(a, 1)
+        ev(b, 0, False)
+        transposes(b)
+        m1(a, 0)
+        m1(a, 1)
+        sq(b, 2)
+        th(a, 0)
+        th(a, 1)
+        m1(b, 2)
+        th(b, 2)
+        for c in (a, b):
+            for m in range(2):
+                m2(c, m)
+        for c in (a, b):
+            for m in range(2):
+                s2(c, m)
+                s3(c, m)
 
         r = keep.tile([P, 6], F32, name="r")
         nc.vector.tensor_reduce(out=r[:], in_=stv[:].rearrange("p w m c -> p (w m) c"), axis=AX.X, op=ALU.add)
-        s1, s3, s2 = r[:, 0:2], r[:, 2:4], r[:, 4:6]
+        s1, s3r, s2r = r[:, 0:2], r[:, 2:4], r[:, 4:6]
         msq = keep.tile([P, 2], F32, name="msq")
         nc.vector.scalar_tensor_tensor(out=msq[:], in0=s1, scalar=-K1 * K1, in1=s1, op0=ALU.mult, op1=ALU.mult)
         var = keep.tile([P, 2], F32, name="var")
-        nc.vector.scalar_tensor_tensor(out=var[:], in0=s2, scalar=K2, in1=msq[:], op0=ALU.mult, op1=ALU.add)
-        sd2 = keep.tile([P, 2], F32, name="sd2")
-        nc.scalar.activation(out=sd2[:], in_=var[:], func=ACT.Sqrt, bias=eps_t[:])
-        num = keep.tile([P, 2], F32, name="num")
-        nc.vector.scalar_tensor_tensor(out=num[:], in0=s1, scalar=cst[:, 0:1], in1=s3, op0=ALU.mult, op1=ALU.add)
+        nc.vector.scalar_tensor_tensor(out=var[:], in0=s2r, scalar=K2, in1=msq[:], op0=ALU.mult, op1=ALU.add)
         rstd = keep.tile([P, 2], F32, name="rstd")
-        nc.vector.reciprocal(out=rstd[:], in_=sd2[:])
-        prod = keep.tile([P, 2], F32, name="prod")
-        nc.vector.tensor_tensor(out=prod[:], in0=num[:], in1=rstd[:], op=ALU.mult)
-        nc.vector.tensor_scalar(
-            out=res[:, 0:2], in0=prod[:], scalar1=cst[:, 1:2], scalar2=0.0, op0=ALU.add, op1=ALU.max
-        )
+        nc.gpsimd.tensor_tensor(out=rstd[:], in0=var[:], in1=nhalf[:], op=ALU.pow)
+        num = keep.tile([P, 2], F32, name="num")
+        nc.vector.scalar_tensor_tensor(out=num[:], in0=s1, scalar=cst[:, 0:1], in1=s3r, op0=ALU.mult, op1=ALU.add)
+        nc.vector.tensor_tensor(out=res[:, 0:2], in0=num[:], in1=rstd[:], op=ALU.mult)
         rps = psum.tile([P, P], F32, tag="bank", name="rps")
         nc.tensor.transpose(rps[:], res[:], ident[:])
         fin = keep.tile([P, P], F32, name="fin")
-        nc.vector.tensor_copy(out=fin[:], in_=rps[:])
+        nc.vector.tensor_scalar(out=fin[:], in0=rps[:], scalar1=cst[:, 1:2], scalar2=0.0, op0=ALU.add, op1=ALU.max)
         nc.sync.dma_start(out=out.rearrange("(m r) o -> m (r o)", m=2), in_=fin[0:2, :])

@@ -33,7 +33,7 @@ CUT = [2, 2, 2, 2]
 HALF = N // 2
 CHUNKS = [4, 4, 4, 4, 4, 4, 4, 3, 1]
 NC = len(CHUNKS)
-WARM = 8
+WARM = 4
 LEAD = 6
 
 
@@ -57,8 +57,6 @@ def tile_modelnew_w_kernel(
         for h in range(2):
             pl = keep.tile([P, 2, HALF], U8, align_bytes=64, name="planes%d" % h)
             planes.append(pl)
-        gwrow = keep.tile([P, N], BF16, name="gwrow")
-        nc.vector.memset(gwrow[:].bitcast(I32), 0)
         nc.vector.memset(planes[0][:].rearrange("p s n -> p (s n)").bitcast(I32), 0)
         nc.vector.memset(planes[1][:].rearrange("p s n -> p (s n)").bitcast(I32), 0)
         vecs = keep.tile([P, 2, P], BF16, name="vecs")
@@ -83,40 +81,43 @@ def tile_modelnew_w_kernel(
         nc.gpsimd.memset(res[:], 0.0)
         nhalf = keep.tile([P, 2], F32, name="nhalf")
         nc.gpsimd.memset(nhalf[:], -0.5)
+        identb = keep.tile([P, P], BF16, name="identb")
+        nc.vector.tensor_copy(out=identb[:], in_=ident[:])
 
         def by_rows(v):
             return v.rearrange("(j p) -> j p", p=P)
 
+        nc.sync.dma_start(out=gv[0:32, 0, :], in_=by_rows(gn_weight))
         for i, v in enumerate([bias, bn_weight, bn_bias, bn_mean, bn_var]):
             r0 = 32 * (i % 4)
-            nc.sync.dma_start(out=vecs[r0 : r0 + 32, i // 4, :], in_=by_rows(v))
+            nc.scalar.dma_start(out=vecs[r0 : r0 + 32, i // 4, :], in_=by_rows(v))
         xv = x.rearrange("(m p) k -> p m k", p=P)
         xs = []
         for q in range(4):
             xq = keep.tile([P, 2, 1024], BF16, name="x%d" % q)
             nc.sync.dma_start(out=xq[:], in_=xv[:, :, 1024 * q : 1024 * (q + 1)])
             xs.append(xq)
-            if q == 0:
-                nc.sync.dma_start(out=gwrow[0:1, :], in_=gn_weight.rearrange("(o n) -> o n", o=1))
 
-        def load_scales(h):
-            for s in range(2):
-                for quad in range(4):
-                    nc.sync.dma_start(
-                        out=planes[h][32 * quad : 32 * quad + 16, s, :].bitcast(I32),
-                        in_=weight_scales[4 * s : 4 * s + 4, 4 * quad : 4 * quad + 4, h * HALF : (h + 1) * HALF].bitcast(I32),
-                    )
+        def load_scales(h, s):
+            for quad in range(4):
+                nc.sync.dma_start(
+                    out=planes[h][32 * quad : 32 * quad + 16, s, :].bitcast(I32),
+                    in_=weight_scales[4 * s : 4 * s + 4, 4 * quad : 4 * quad + 4, h * HALF : (h + 1) * HALF].bitcast(I32),
+                )
 
         wv = weight_words.rearrange("g p n t -> p g (n t)")
         where = {}
-        load_scales(0)
+        load_scales(0, 0)
         for d in range(LOADS):
             if d * LOAD_TILES * P == HALF:
-                load_scales(1)
+                load_scales(1, 0)
+                load_scales(1, 1)
             cols = LOAD_TILES * P
             n0 = d * cols
             g0 = 0
             for i, gd in enumerate(FIRST_CUT if d == 0 else CUT):
+                if d == 0 and g0 == 4:
+                    load_scales(0, 1)
                 wt = keep.tile([P, gd, cols], U32, align_bytes=64, name="w%d_%d" % (d, i))
                 nc.sync.dma_start(
                     out=wt[:].bitcast(I32), in_=wv[:, g0 : g0 + gd, 4 * n0 : 4 * (n0 + cols)].bitcast(I32)
@@ -125,7 +126,6 @@ def tile_modelnew_w_kernel(
                     where[(d, g)] = (wt, g - g0)
                 g0 += gd
             if d == 0:
-                nc.sync.dma_start(out=gv[0:32, 0, :], in_=by_rows(gn_weight))
                 nc.sync.dma_start(out=gv[0:32, 1, :], in_=by_rows(gn_bias))
 
         junk0 = keep.tile([P, 1], F32, name="junk0")
@@ -135,22 +135,19 @@ def tile_modelnew_w_kernel(
         xsc = keep.tile([P, PASSES, ROWS], U8, align_bytes=64, name="xsc")
         vecf = keep.tile([P, 2, P], F32, name="vecf")
         gwbc = keep.tile([P, N], BF16, name="gwbc")
+        nc.vector.tensor_copy(out=vecf[:], in_=vecs[:])
         idle = psum.tile([P, 512], F32, tag="bank", name="idle")
         for i in range(WARM):
             nc.tensor.matmul(out=idle[:], lhsT=ones_bf[:], rhs=warm[:], start=True, stop=True)
-        gpss = []
-
-        def spread(i):
-            if i % 2 == 0:
-                gps = psum.tile([P, 1024], BF16, tag="bank", name="gps%d" % (i // 2))
-                gpss.append(gps)
-            half = (i % 2) * 512
-            nc.tensor.matmul(
-                out=gpss[i // 2][:, half : half + 512], lhsT=ones_bf[:], rhs=gwrow[:, i * 512 : (i + 1) * 512],
-                start=True, stop=True,
-            )
-            if i % 2 == 1:
-                nc.vector.tensor_copy(out=gwbc[:, (i - 1) * 512 : (i + 1) * 512], in_=gpss[i // 2][:])
+        for i in range(4):
+            gps = psum.tile([P, 1024], BF16, tag="bank", name="gps%d" % i)
+            for jj in range(8):
+                j = 8 * i + jj
+                nc.tensor.matmul(
+                    out=gps[:, jj * P : (jj + 1) * P], lhsT=identb[:, j : j + 1].to_broadcast([P, P]), rhs=gv[:, 0, :],
+                    start=True, stop=True,
+                )
+            nc.vector.tensor_copy(out=gwbc[:, i * 1024 : (i + 1) * 1024], in_=gps[:])
 
         for g in range(PASSES):
             xt = psum.tile([P, 2, ROWS], F32, tag="bank", name="xt%d" % g)
@@ -165,12 +162,6 @@ def tile_modelnew_w_kernel(
                 in_=xt[:].rearrange("p u r -> p r u"),
             )
             nc.vector.quantize_mx(out=xc[:, g, :].bitcast(FP8X4), scales=xsc[:, g, :], in_=grp[:])
-            if g == 0:
-                nc.vector.tensor_copy(out=vecf[:], in_=vecs[:])
-                nc.tensor.matmul(out=idle[:], lhsT=ones_bf[:], rhs=warm[:], start=True, stop=True)
-            else:
-                spread(g - 1)
-        spread(PASSES - 1)
 
         vps = psum.tile([P, 2, P], F32, tag="bank", name="vps")
         for h in range(2):
@@ -296,7 +287,7 @@ def tile_modelnew_w_kernel(
             w = CHUNKS[c] * P
             n0 = starts[c] * P
             nc.vector.scalar_tensor_tensor(
-                out=junk_v[:, :w], in0=es[c][m], scalar=1.0, in1=gwbc[:, n0 : n0 + w], op0=ALU.mult, op1=ALU.mult,
+                out=junk_v[:, :w], in0=es[c][m], scalar=K1, in1=gwbc[:, n0 : n0 + w], op0=ALU.mult, op1=ALU.mult,
                 accum_out=stv[:, 1, m, c : c + 1],
             )
 

@@ -24,6 +24,7 @@ C2 = 0.035677
 KAPPA = C1 / C2
 K1 = 1.0 / (2 * N)
 K2 = 1.0 / (4 * N)
+RS = (4 * N) ** 0.5
 FLOPS = 2 * ROWS * K * N
 
 LOAD_TILES = 4
@@ -65,9 +66,9 @@ def tile_modelnew_w_kernel(
         gv = keep.tile([P, 2, P], BF16, name="gv")
         nc.vector.memset(gv[32:64, :, :], 0.0)
         nc.vector.memset(gv[64:128, :, :], 0.0)
-        stv = keep.tile([P, 3, 2, NC + 1], F32, name="stv")
+        stv = keep.tile([P, 3, 2, NC + 2], F32, name="stv")
         nc.vector.memset(stv[:], 0.0)
-        nc.vector.memset(stv[:, 2, :, NC : NC + 1], EPS / K2)
+        nc.vector.memset(stv[:, 1, :, NC : NC + 1], EPS / K2)
 
         ones_bf = keep.tile([P, P], BF16, name="ones_bf")
         nc.gpsimd.memset(ones_bf[:], K1)
@@ -281,14 +282,23 @@ def tile_modelnew_w_kernel(
 
         def s2(c, m):
             w = CHUNKS[c] * P
-            nc.scalar.activation(out=junk_s[:, :w], in_=es[c][m], func=ACT.Square, accum_out=stv[:, 2, m, c : c + 1])
+            nc.scalar.activation(out=junk_s[:, :w], in_=es[c][m], func=ACT.Square, accum_out=stv[:, 1, m, c : c + 1])
 
         def s3(c, m):
             w = CHUNKS[c] * P
             n0 = starts[c] * P
             nc.vector.scalar_tensor_tensor(
-                out=junk_v[:, :w], in0=es[c][m], scalar=K1, in1=gwbc[:, n0 : n0 + w], op0=ALU.mult, op1=ALU.mult,
-                accum_out=stv[:, 1, m, c : c + 1],
+                out=junk_v[:, :w], in0=es[c][m], scalar=K1 * RS, in1=gwbc[:, n0 : n0 + w], op0=ALU.mult, op1=ALU.mult,
+                accum_out=stv[:, 2, m, c : c + 1],
+            )
+
+        def s3_beside(c, m):
+            w = CHUNKS[c] * P
+            n0 = starts[c] * P
+            prod = work.tile([P, 512], F32, tag="prod", bufs=2, name="prod%d_%d" % (c, m))
+            nc.gpsimd.tensor_tensor(out=prod[:, :w], in0=es[c][m], in1=gwbc[:, n0 : n0 + w], op=ALU.mult)
+            nc.scalar.activation(
+                out=junk_s[:, :w], in_=prod[:, :w], func=ACT.Identity, scale=K1 * RS, accum_out=stv[:, 2, m, c : c + 1]
             )
 
         def mainops(c):
@@ -314,7 +324,7 @@ def tile_modelnew_w_kernel(
                 tailops(c - 1)
             mainops(c)
             if c == 1:
-                nc.vector.tensor_scalar(out=cst[:, 0:1], in0=cps[:, 0:1], scalar1=-K1, scalar2=None, op0=ALU.mult)
+                nc.vector.tensor_scalar(out=cst[:, 0:1], in0=cps[:, 0:1], scalar1=-K1 * RS, scalar2=None, op0=ALU.mult)
                 nc.vector.tensor_copy(out=cst[:, 1:2], in_=cps[:, 1:2])
             passes(c + 1, pass_order(c + 1)[LEAD:])
 
@@ -339,23 +349,26 @@ def tile_modelnew_w_kernel(
         for c in (a, b):
             for m in range(2):
                 m2(c, m)
+        r = keep.tile([P, 6], F32, name="r")
+        sums = stv[:].rearrange("p w m c -> p (w m) c")
+        s1, s2r, s3r = r[:, 0:2], r[:, 2:4], r[:, 4:6]
         for c in (a, b):
             for m in range(2):
                 s2(c, m)
-                s3(c, m)
-
-        r = keep.tile([P, 6], F32, name="r")
-        nc.vector.tensor_reduce(out=r[:], in_=stv[:].rearrange("p w m c -> p (w m) c"), axis=AX.X, op=ALU.add)
-        s1, s3r, s2r = r[:, 0:2], r[:, 2:4], r[:, 4:6]
-        msq = keep.tile([P, 2], F32, name="msq")
-        nc.vector.scalar_tensor_tensor(out=msq[:], in0=s1, scalar=-K1 * K1, in1=s1, op0=ALU.mult, op1=ALU.mult)
-        var = keep.tile([P, 2], F32, name="var")
-        nc.vector.scalar_tensor_tensor(out=var[:], in0=s2r, scalar=K2, in1=msq[:], op0=ALU.mult, op1=ALU.add)
+        s3_beside(a, 0)
+        s3_beside(a, 1)
+        nc.vector.tensor_reduce(out=s1, in_=sums[:, 0:2, :], axis=AX.X, op=ALU.add)
+        nc.vector.scalar_tensor_tensor(
+            out=stv[:, 1, :, NC + 1], in0=s1, scalar=-K1 * K1 / K2, in1=s1, op0=ALU.mult, op1=ALU.mult
+        )
+        nc.vector.tensor_scalar(out=stv[:, 2, :, NC + 1], in0=s1, scalar1=cst[:, 0:1], scalar2=None, op0=ALU.mult)
+        s3(b, 0)
+        s3(b, 1)
+        nc.vector.tensor_reduce(out=s2r, in_=sums[:, 2:4, :], axis=AX.X, op=ALU.add)
         rstd = keep.tile([P, 2], F32, name="rstd")
-        nc.gpsimd.tensor_tensor(out=rstd[:], in0=var[:], in1=nhalf[:], op=ALU.pow)
-        num = keep.tile([P, 2], F32, name="num")
-        nc.vector.scalar_tensor_tensor(out=num[:], in0=s1, scalar=cst[:, 0:1], in1=s3r, op0=ALU.mult, op1=ALU.add)
-        nc.vector.tensor_tensor(out=res[:, 0:2], in0=num[:], in1=rstd[:], op=ALU.mult)
+        nc.gpsimd.tensor_tensor(out=rstd[:], in0=s2r, in1=nhalf[:], op=ALU.pow)
+        nc.vector.tensor_reduce(out=s3r, in_=sums[:, 4:6, :], axis=AX.X, op=ALU.add)
+        nc.vector.tensor_tensor(out=res[:, 0:2], in0=s3r, in1=rstd[:], op=ALU.mult)
         rps = psum.tile([P, P], F32, tag="bank", name="rps")
         nc.tensor.transpose(rps[:], res[:], ident[:])
         fin = keep.tile([P, P], F32, name="fin")

from contextlib import ExitStack

import concourse.mybir as mybir
from concourse.masks import make_identity

F32 = mybir.dt.float32
BF16 = mybir.dt.bfloat16
U8 = mybir.dt.uint8
U32 = mybir.dt.uint32
I32 = mybir.dt.int32
FP8X4 = mybir.dt.float8_e4m3fn_x4
ACT = mybir.ActivationFunctionType
ALU = mybir.AluOpType
AX = mybir.AxisListType

P = 128
ROWS = 256
K = 4096
N = 4096
PASSES = K // 512
EPS = 1e-5
C1 = 0.797885
C2 = 0.035677
KAPPA = C1 / C2
K1 = 1.0 / (2 * N)
K2 = 1.0 / (4 * N)
RS = (4 * N) ** 0.5
FLOPS = 2 * ROWS * K * N

LOAD_TILES = 4
LOADS = N // (P * LOAD_TILES)
FIRST_CUT = [1, 1, 2, 2, 2]
CUT = [2, 2, 2, 2]
HALF = N // 2
CHUNKS = [4, 4, 4, 4, 4, 4, 4, 3, 1]
NC = len(CHUNKS)
WARM = 4
LEAD = 6


def tile_modelnew_w_kernel(
    tc, x, weight_words, weight_scales, bias, bn_weight, bn_bias, bn_mean, bn_var, gn_weight, gn_bias, out
):
    nc = tc.nc
    assert sum(CHUNKS) * P == N
    starts = [sum(CHUNKS[:c]) for c in range(NC)]
    with ExitStack() as ctx:
        ctx.enter_context(tc.manual_schedule())
        keep = ctx.enter_context(tc.tile_pool(name="keep", bufs=1))
        work = ctx.enter_context(tc.tile_pool(name="work", bufs=3))
        psum = ctx.enter_context(tc.psum_pool(name="psum", bufs=8))

        one = keep.tile([P, 1], F32, name="one")
        nc.vector.memset(one[:], 1.0)
        eps_t = keep.tile([P, 1], F32, name="eps_t")
        nc.vector.memset(eps_t[:], EPS)
        planes = []
        for h in range(2):
            pl = keep.tile([P, 2, HALF], U8, align_bytes=64, name="planes%d" % h)
            planes.append(pl)
        nc.vector.memset(planes[0][:].rearrange("p s n -> p (s n)").bitcast(I32), 0)
        nc.vector.memset(planes[1][:].rearrange("p s n -> p (s n)").bitcast(I32), 0)
        vecs = keep.tile([P, 2, P], BF16, name="vecs")
        nc.vector.memset(vecs[32:64, 1, :], 0.0)
        nc.vector.memset(vecs[64:128, 1, :], 0.0)
        gv = keep.tile([P, 2, P], BF16, name="gv")
        nc.vector.memset(gv[32:64, :, :], 0.0)
        nc.vector.memset(gv[64:128, :, :], 0.0)
        stv = keep.tile([P, 3, 2, NC + 2], F32, name="stv")
        nc.vector.memset(stv[:], 0.0)
        nc.vector.memset(stv[:, 1, :, NC : NC + 1], EPS / K2)

        ones_bf = keep.tile([P, P], BF16, name="ones_bf")
        nc.gpsimd.memset(ones_bf[:], K1)
        warm = keep.tile([P, 512], BF16, name="warm")
        nc.gpsimd.memset(warm[:], 0.0)
        ident = keep.tile([P, P], F32, name="ident")
        make_identity(nc, ident[:])
        ones_n = keep.tile([P, P], F32, name="ones_n")
        nc.gpsimd.memset(ones_n[:], 1.0 / N)
        res = keep.tile([P, P], F32, name="res")
        nc.gpsimd.memset(res[:], 0.0)
        nhalf = keep.tile([P, 2], F32, name="nhalf")
        nc.gpsimd.memset(nhalf[:], -0.5)
        identb = keep.tile([P, P], BF16, name="identb")
        nc.vector.tensor_copy(out=identb[:], in_=ident[:])

        def by_rows(v):
            return v.rearrange("(j p) -> j p", p=P)

        nc.sync.dma_start(out=gv[0:32, 0, :], in_=by_rows(gn_weight))
        for i, v in enumerate([bias, bn_weight, bn_bias, bn_mean, bn_var]):
            r0 = 32 * (i % 4)
            nc.scalar.dma_start(out=vecs[r0 : r0 + 32, i // 4, :], in_=by_rows(v))
        xv = x.rearrange("(m p) k -> p m k", p=P)
        xs = []
        for q in range(4):
            xq = keep.tile([P, 2, 1024], BF16, name="x%d" % q)
            nc.sync.dma_start(out=xq[:], in_=xv[:, :, 1024 * q : 1024 * (q + 1)])
            xs.append(xq)

        def load_scales(h, s):
            for quad in range(4):
                nc.sync.dma_start(
                    out=planes[h][32 * quad : 32 * quad + 16, s, :].bitcast(I32),
                    in_=weight_scales[4 * s : 4 * s + 4, 4 * quad : 4 * quad + 4, h * HALF : (h + 1) * HALF].bitcast(I32),
                )

        wv = weight_words.rearrange("g p n t -> p g (n t)")
        where = {}
        load_scales(0, 0)
        for d in range(LOADS):
            if d * LOAD_TILES * P == HALF:
                load_scales(1, 0)
                load_scales(1, 1)
            cols = LOAD_TILES * P
            n0 = d * cols
            g0 = 0
            for i, gd in enumerate(FIRST_CUT if d == 0 else CUT):
                if d == 0 and g0 == 4:
                    load_scales(0, 1)
                wt = keep.tile([P, gd, cols], U32, align_bytes=64, name="w%d_%d" % (d, i))
                nc.sync.dma_start(
                    out=wt[:].bitcast(I32), in_=wv[:, g0 : g0 + gd, 4 * n0 : 4 * (n0 + cols)].bitcast(I32)
                )
                for g in range(g0, g0 + gd):
                    where[(d, g)] = (wt, g - g0)
                g0 += gd
            if d == 0:
                nc.sync.dma_start(out=gv[0:32, 1, :], in_=by_rows(gn_bias))

        junk0 = keep.tile([P, 1], F32, name="junk0")
        nc.scalar.activation(out=junk0[:], in_=one[:], func=ACT.Sqrt)

        xc = keep.tile([P, PASSES, ROWS], U32, align_bytes=64, name="xc")
        xsc = keep.tile([P, PASSES, ROWS], U8, align_bytes=64, name="xsc")
        vecf = keep.tile([P, 2, P], F32, name="vecf")
        gwbc = keep.tile([P, N], BF16, name="gwbc")
        nc.vector.tensor_copy(out=vecf[:], in_=vecs[:])
        idle = psum.tile([P, 512], F32, tag="bank", name="idle")
        for i in range(WARM):
            nc.tensor.matmul(out=idle[:], lhsT=ones_bf[:], rhs=warm[:], start=True, stop=True)
        for i in range(4):
            gps = psum.tile([P, 1024], BF16, tag="bank", name="gps%d" % i)
            for jj in range(8):
                j = 8 * i + jj
                nc.tensor.matmul(
                    out=gps[:, jj * P : (jj + 1) * P], lhsT=identb[:, j : j + 1].to_broadcast([P, P]), rhs=gv[:, 0, :],
                    start=True, stop=True,
                )
            nc.vector.tensor_copy(out=gwbc[:, i * 1024 : (i + 1) * 1024], in_=gps[:])

        for g in range(PASSES):
            xt = psum.tile([P, 2, ROWS], F32, tag="bank", name="xt%d" % g)
            for m in range(2):
                words = xs[g // 2][:, m, :].bitcast(F32)
                base = 256 * (g % 2)
                for u in range(2):
                    nc.tensor.transpose(xt[:, u, m * P : (m + 1) * P], words[:, base + u : base + 256 : 2], ident[:])
            grp = work.tile([P, 4 * ROWS], BF16, align_bytes=64, tag="grp", name="grp%d" % g)
            nc.scalar.copy(
                out=grp[:].bitcast(F32).rearrange("p (r u) -> p r u", u=2),
                in_=xt[:].rearrange("p u r -> p r u"),
            )
            nc.vector.quantize_mx(out=xc[:, g, :].bitcast(FP8X4), scales=xsc[:, g, :], in_=grp[:])

        vps = psum.tile([P, 2, P], F32, tag="bank", name="vps")
        for h in range(2):
            nc.tensor.transpose(vps[:, h, :], vecf[:, h, :], ident[:])
        vt = keep.tile([P, 160], F32, name="vt")
        nc.vector.tensor_copy(out=vt[:], in_=vps[:].rearrange("p h j -> p (h j)")[:, 0:160])
        v_bias, v_bnw, v_bnb, v_bnm, v_var = vt[:, 0:32], vt[:, 32:64], vt[:, 64:96], vt[:, 96:128], vt[:, 128:160]
        sd = keep.tile([P, 32], F32, name="sd")
        nc.scalar.activation(out=sd[:], in_=v_var, func=ACT.Sqrt, bias=eps_t[:])
        junk1 = keep.tile([P, 1], F32, name="junk1")
        nc.scalar.activation(out=junk1[:], in_=sd[:, 0:1], func=ACT.Tanh)
        gd0 = keep.tile([P, 32], F32, name="gd0")
        nc.vector.tensor_tensor(out=gd0[:], in0=v_bias, in1=v_bnm, op=ALU.subtract)
        rs = keep.tile([P, 32], F32, name="rs")
        nc.vector.reciprocal(out=rs[:], in_=sd[:])
        ga = keep.tile([P, 32], F32, name="ga")
        nc.vector.tensor_tensor(out=ga[:], in0=v_bnw, in1=rs[:], op=ALU.mult)
        gd1 = keep.tile([P, 32], F32, name="gd1")
        nc.vector.tensor_tensor(out=gd1[:], in0=gd0[:], in1=ga[:], op=ALU.mult)
        gb = keep.tile([P, 32], F32, name="gb")
        nc.vector.tensor_tensor(out=gb[:], in0=gd1[:], in1=v_bnb, op=ALU.add)

        junk_s = keep.tile([P, 512], F32, name="junk_s")
        junk_v = keep.tile([P, 512], F32, name="junk_v")
        gsum = keep.tile([P, 2], F32, name="gsum")
        cst = keep.tile([P, 2], F32, name="cst")
        mx = {}
        zs = {}
        zts = {}
        es = {}

        def pass_order(c):
            tiles = CHUNKS[c]
            early = [(g, t) for g in range(PASSES - 2) for t in range(tiles)]
            late = [(g, t) for t in range(tiles) for g in (PASSES - 2, PASSES - 1)]
            return early + late

        def passes(c, todo):
            if c not in mx:
                banks = []
                for t in range(CHUNKS[c]):
                    bank = psum.tile([P, ROWS], F32, tag="bank", name="mx%d_%d" % (c, t))
                    banks.append(bank)
                mx[c] = banks
            for g, t in todo:
                j = starts[c] + t
                wt, gi = where[(j // LOAD_TILES, g)]
                lo = (j % LOAD_TILES) * P
                s, kk = divmod(g, 4)
                n0 = (j * P) % HALF
                nc.tensor.matmul_mx(
                    out=mx[c][t][:],
                    lhsT=wt[:, gi, lo : lo + P].bitcast(FP8X4),
                    lhsT_scale=planes[(j * P) // HALF][4 * kk : P, s, n0 : n0 + P],
                    rhs=xc[:, g, :].bitcast(FP8X4),
                    rhs_scale=xsc[:, g, :],
                    start=(g == 0),
                    stop=(g == PASSES - 1),
                )

        def ev(c, t, on_scalar):
            j = starts[c] + t
            z = work.tile([P, ROWS], F32, tag="z", bufs=8, name="z%d" % j)
            if on_scalar:
                nc.scalar.activation(
                    out=z[:], in_=mx[c][t][:], func=ACT.Identity, bias=gb[:, j : j + 1], scale=ga[:, j : j + 1]
                )
            else:
                nc.vector.tensor_scalar(
                    out=z[:], in0=mx[c][t][:], scalar1=ga[:, j : j + 1], scalar2=gb[:, j : j + 1],
                    op0=ALU.mult, op1=ALU.add,
                )
            zs.setdefault(c, []).append(z)

        def evac(c):
            for t in range(CHUNKS[c]):
                ev(c, t, t % 2 == 0)

        def joint(c):
            return 2 * CHUNKS[c] * P <= 512

        def transposes(c):
            w = CHUNKS[c] * P
            if joint(c):
                zt = psum.tile([P, 512], F32, tag="bank", name="zt%d" % c)
                e = work.tile([P, 512], F32, tag="e", bufs=6, name="e%d" % c)
                zts[c] = [zt[:, m * w : (m + 1) * w] for m in range(2)] + [zt[:, : 2 * w]]
                es[c] = [e[:, m * w : (m + 1) * w] for m in range(2)] + [e[:, : 2 * w]]
            else:
                zts[c] = []
                es[c] = []
                for m in range(2):
                    zt = psum.tile([P, 512], F32, tag="bank", name="zt%d_%d" % (c, m))
                    e = work.tile([P, 512], F32, tag="e", bufs=6, name="e%d_%d" % (c, m))
                    zts[c].append(zt[:, :w])
                    es[c].append(e[:, :w])
            for m in range(2):
                for t in range(CHUNKS[c]):
                    nc.tensor.transpose(zts[c][m][:, t * P : (t + 1) * P], zs[c][t][:, m * P : (m + 1) * P], ident[:])

        def sq(c, m):
            nc.scalar.activation(out=es[c][m], in_=zts[c][m], func=ACT.Square)

        def m1(c, m):
            nc.vector.scalar_tensor_tensor(
                out=es[c][m], in0=es[c][m], scalar=KAPPA, in1=zts[c][m], op0=ALU.add, op1=ALU.mult
            )

        def th(c, m):
            nc.scalar.activation(out=es[c][m], in_=es[c][m], func=ACT.Tanh, scale=C2)

        def m2(c, m):
            nc.vector.scalar_tensor_tensor(
                out=es[c][m], in0=es[c][m], scalar=1.0, in1=zts[c][m], op0=ALU.add, op1=ALU.mult,
                accum_out=stv[:, 0, m, c : c + 1],
            )

        def s2(c, m):
            w = CHUNKS[c] * P
            nc.scalar.activation(out=junk_s[:, :w], in_=es[c][m], func=ACT.Square, accum_out=stv[:, 1, m, c : c + 1])

        def s3(c, m):
            w = CHUNKS[c] * P
            n0 = starts[c] * P
            nc.vector.scalar_tensor_tensor(
                out=junk_v[:, :w], in0=es[c][m], scalar=K1 * RS, in1=gwbc[:, n0 : n0 + w], op0=ALU.mult, op1=ALU.mult,
                accum_out=stv[:, 2, m, c : c + 1],
            )

        def s3_beside(c, m):
            w = CHUNKS[c] * P
            n0 = starts[c] * P
            prod = work.tile([P, 512], F32, tag="prod", bufs=2, name="prod%d_%d" % (c, m))
            nc.gpsimd.tensor_tensor(out=prod[:, :w], in0=es[c][m], in1=gwbc[:, n0 : n0 + w], op=ALU.mult)
            nc.scalar.activation(
                out=junk_s[:, :w], in_=prod[:, :w], func=ACT.Identity, scale=K1 * RS, accum_out=stv[:, 2, m, c : c + 1]
            )

        def mainops(c):
            for step in (sq, m1, th, m2):
                for m in range(2):
                    step(c, m)

        def tailops(c):
            for m in range(2):
                s2(c, m)
                s3(c, m)

        passes(0, pass_order(0))
        for c in range(NC - 2):
            evac(c)
            passes(c + 1, pass_order(c + 1)[:LEAD])
            transposes(c)
            if c == 1:
                nc.vector.tensor_reduce(out=gsum[:], in_=gv[:], axis=AX.X, op=ALU.add)
                cps = psum.tile([P, 2], F32, tag="bank", name="cps")
                nc.tensor.matmul(out=cps[:], lhsT=ones_n[:], rhs=gsum[:], start=True, stop=True)
            if c >= 1:
                tailops(c - 1)
            mainops(c)
            if c == 1:
                nc.vector.tensor_scalar(out=cst[:, 0:1], in0=cps[:, 0:1], scalar1=-K1 * RS, scalar2=None, op0=ALU.mult)
                nc.vector.tensor_copy(out=cst[:, 1:2], in_=cps[:, 1:2])
            passes(c + 1, pass_order(c + 1)[LEAD:])

        a, b = NC - 2, NC - 1
        assert joint(b) and CHUNKS[b] == 1
        evac(a)
        passes(b, pass_order(b)[:LEAD])
        transposes(a)
        passes(b, pass_order(b)[LEAD:])
        tailops(a - 1)
        sq(a, 0)
        sq(a, 1)
        ev(b, 0, False)
        transposes(b)
        m1(a, 0)
        m1(a, 1)
        sq(b, 2)
        th(a, 0)
        th(a, 1)
        m1(b, 2)
        th(b, 2)
        for c in (a, b):
            for m in range(2):
                m2(c, m)
        r = keep.tile([P, 6], F32, name="r")
        sums = stv[:].rearrange("p w m c -> p (w m) c")
        s1, s2r, s3r = r[:, 0:2], r[:, 2:4], r[:, 4:6]
        for c in (a, b):
            for m in range(2):
                s2(c, m)
        s3_beside(a, 0)
        s3_beside(a, 1)
        nc.vector.tensor_reduce(out=s1, in_=sums[:, 0:2, :], axis=AX.X, op=ALU.add)
        nc.vector.scalar_tensor_tensor(
            out=stv[:, 1, :, NC + 1], in0=s1, scalar=-K1 * K1 / K2, in1=s1, op0=ALU.mult, op1=ALU.mult
        )
        nc.vector.tensor_scalar(out=stv[:, 2, :, NC + 1], in0=s1, scalar1=cst[:, 0:1], scalar2=None, op0=ALU.mult)
        s3(b, 0)
        s3(b, 1)
        nc.vector.tensor_reduce(out=s2r, in_=sums[:, 2:4, :], axis=AX.X, op=ALU.add)
        rstd = keep.tile([P, 2], F32, name="rstd")
        nc.gpsimd.tensor_tensor(out=rstd[:], in0=s2r, in1=nhalf[:], op=ALU.pow)
        nc.vector.tensor_reduce(out=s3r, in_=sums[:, 4:6, :], axis=AX.X, op=ALU.add)
        nc.vector.tensor_tensor(out=res[:, 0:2], in0=s3r, in1=rstd[:], op=ALU.mult)
        rps = psum.tile([P, P], F32, tag="bank", name="rps")
        nc.tensor.transpose(rps[:], res[:], ident[:])
        fin = keep.tile([P, P], F32, name="fin")
        nc.vector.tensor_scalar(out=fin[:], in0=rps[:], scalar1=cst[:, 1:2], scalar2=0.0, op0=ALU.add, op1=ALU.max)
        nc.sync.dma_start(out=out.rearrange("(m r) o -> m (r o)", m=2), in_=fin[0:2, :])
